import numpy as np
import ml_dtypes


def mxq(x, axis, fmt="e4m3"):
    dtype, down = {"e4m3": (ml_dtypes.float8_e4m3fn, 7), "e5m2": (ml_dtypes.float8_e5m2, 14)}[fmt]
    v = np.moveaxis(np.asarray(x, np.float32).astype(ml_dtypes.bfloat16).astype(np.float64), axis, -1)
    blocks = v.reshape(v.shape[:-1] + (-1, 32))
    amax = np.abs(blocks).max(-1, keepdims=True)
    byte = np.maximum(np.where(amax > 0, np.frexp(amax)[1] - 1 + 127, 0) - down, 1)
    scale = np.exp2(byte - 127.0)
    codes = (blocks / scale).astype(np.float32).astype(dtype).astype(np.float64)
    return np.moveaxis((codes * scale).reshape(v.shape), -1, axis)


WIDE = False


def mx_kscale(k):
    if not WIDE:
        return np.ones(k)
    levels = np.array([10, -10, 5, -5, 0])
    a = np.random.permutation(np.resize(levels, k // 512 * 4)).reshape(k // 512, 4)
    idx = np.arange(k)
    return np.exp2(a[idx // 512, idx % 128 // 32])


BF16 = ml_dtypes.bfloat16


def bf(x):
    return np.asarray(x, np.float32).astype(BF16)


def f64(x):
    return np.asarray(x).astype(np.float64)


B, F, C, DEPTH, LQ = 8192, 1024, 128, 10, 7
NL = 2 ** (DEPTH - 1)
NQ = 2 ** LQ


def sigmoid(v):
    return 1.0 / (1.0 + np.exp(-v))


def setup_inputs():
    s = mx_kscale(F)
    return {"x": bf(np.random.standard_normal((B, F)) * s),
            "W_gate": bf(np.random.standard_normal((F, NL - 1)) * 2.0 / np.sqrt(F) / s[:, None]),
            "b_gate": bf(np.random.standard_normal(NL - 1) * 0.5),
            "leaf_logits": bf(np.random.standard_normal((NL, C)) * 0.5 * 1.2 ** (DEPTH - 1))}


def reference(x, W_gate, b_gate, leaf_logits):
    nb = x.shape[0]
    xf, wf = f64(x), f64(W_gate)
    top = (xf @ wf[:, :NQ])[:, :NQ - 1]
    low = mxq(xf, 1, "e4m3") @ mxq(wf[:, NQ - 1:], 0, "e4m3")
    p = sigmoid(np.concatenate([top, low], axis=1) + f64(b_gate))
    probs = np.ones((nb, 1))
    for level in range(DEPTH - 1):
        n = 2 ** level
        start = n - 1
        pl = p[:, start:start + n]
        probs = np.stack([(1.0 - pl) * probs, pl * probs], axis=-1).reshape(nb, 2 * n)
    return mxq(probs, 1, "e4m3") @ mxq(f64(leaf_logits), 0, "e4m3")

@@ -1,0 +1,225 @@
+import concourse.mybir as mybir
+from concourse.masks import make_identity
+
+F32 = mybir.dt.float32
+BF16 = mybir.dt.bfloat16
+U32 = mybir.dt.uint32
+U8 = mybir.dt.uint8
+FP8X4 = mybir.dt.float8_e4m3fn_x4
+SIGMOID = mybir.ActivationFunctionType.Sigmoid
+MULT = mybir.AluOpType.mult
+SUBTRACT = mybir.AluOpType.subtract
+
+P = 128
+BATCH = 8192
+FEATURES = 1024
+NODES = 511
+LEAVES = 512
+CLASSES = 128
+TOP = 128
+TOP_LEVELS = 7
+ROWS = 4
+CHUNK = P * ROWS
+N_CHUNKS = BATCH // CHUNK
+WORD_BLOCKS = 4
+PASSES = 2
+LOW_TILES = 3
+
+FLOPS = 2 * BATCH * FEATURES * (TOP + NODES - TOP + 1) + 2 * BATCH * LEAVES * CLASSES
+
+
+def tile_treemodel_t_kernel(tc, x, w_gate, b_gate, leaf_logits, out):
+    nc = tc.nc
+    x_chunks = x.rearrange("(i p r) k -> i p (r k)", p=P, r=ROWS)
+    out_chunks = out.rearrange("(i p r) c -> i p (r c)", p=P, r=ROWS)
+
+    with tc.tile_pool(name="const", bufs=1) as const, tc.tile_pool(name="setup", bufs=1) as setup, tc.tile_pool(
+        name="stream", bufs=3
+    ) as stream, tc.tile_pool(name="work", bufs=2) as work, tc.psum_pool(name="ps_x", bufs=2) as ps_x, tc.psum_pool(
+        name="ps_top", bufs=1
+    ) as ps_top, tc.psum_pool(name="ps_low", bufs=3) as ps_low, tc.psum_pool(name="ps_p7", bufs=1) as ps_p7, tc.psum_pool(
+        name="ps_out", bufs=1
+    ) as ps_out:
+        ident = const.tile([P, P], F32)
+        make_identity(nc, ident[:])
+        ones = const.tile([P, P], BF16)
+        nc.vector.memset(ones[:], 1.0)
+
+        bias_row = const.tile([P, LEAVES], BF16)
+        nc.vector.memset(bias_row[:], 0.0)
+        nc.sync.dma_start(out=bias_row[0:1, 0:NODES], in_=b_gate.unsqueeze(0))
+
+        w_sb = setup.tile([P, WORD_BLOCKS, 2 * NODES], BF16)
+        nc.sync.dma_start(out=w_sb[:], in_=w_gate.rearrange("(w p e) n -> p w (e n)", w=WORD_BLOCKS, p=P, e=2))
+        w_view = w_sb[:].rearrange("p w (e n) -> p w e n", e=2)
+        leaf_sb = setup.tile([P, 4, CLASSES], BF16)
+        nc.sync.dma_start(out=leaf_sb[:], in_=leaf_logits.rearrange("(p t) c -> p t c", t=4))
+
+        w_top = const.tile([P, WORD_BLOCKS, 2, TOP], BF16)
+        nc.vector.tensor_copy(out=w_top[:], in_=w_view[:, :, :, 0:TOP])
+
+        w_grouped = setup.tile([P, PASSES, LOW_TILES, 4 * P], BF16, align_bytes=64)
+        w_codes = const.tile([P, PASSES, LOW_TILES, P], U32, align_bytes=64)
+        w_scales = const.tile([P, PASSES, LOW_TILES, P], U8, align_bytes=64)
+        low_columns = [slice(127, 255), slice(255, 511, 2), slice(256, 511, 2)]
+        for g in range(PASSES):
+            for nt in range(LOW_TILES):
+                nc.vector.tensor_copy(
+                    out=w_grouped[:, g, nt, :].rearrange("p (m u e) -> p m u e", u=2, e=2),
+                    in_=w_view[:, 2 * g : 2 * g + 2, :, low_columns[nt]].rearrange("p u e m -> p m u e"),
+                )
+        for g in range(PASSES):
+            for nt in range(LOW_TILES):
+                nc.vector.quantize_mx(
+                    out=w_codes[:, g, nt, :].bitcast(FP8X4), scales=w_scales[:, g, nt, :], in_=w_grouped[:, g, nt, :]
+                )
+
+        leaf_grouped = setup.tile([P, CLASSES, 4], BF16, align_bytes=64)
+        nc.vector.tensor_copy(out=leaf_grouped[:], in_=leaf_sb[:].rearrange("p t c -> p c t"))
+        leaf_codes = const.tile([P, CLASSES], U32, align_bytes=64)
+        leaf_scales = const.tile([P, CLASSES], U8, align_bytes=64)
+        nc.vector.quantize_mx(
+            out=leaf_codes[:].bitcast(FP8X4), scales=leaf_scales[:], in_=leaf_grouped[:].rearrange("p c t -> p (c t)")
+        )
+
+        bias_sel = setup.tile([P, LOW_TILES, P], F32)
+        nc.vector.tensor_copy(out=bias_sel[:, 0, :], in_=bias_row[:, 127:255])
+        nc.vector.tensor_copy(out=bias_sel[:, 1:3, :], in_=bias_row[:, 255:511].rearrange("p (m c) -> p c m", c=2))
+        bias_t = ps_low.tile([P, LOW_TILES, P], F32, tag="z_low")
+        for nt in range(LOW_TILES):
+            nc.tensor.transpose(bias_t[:, nt, :], bias_sel[:, nt, :], ident[:])
+        bias_pos = const.tile([P, LOW_TILES], F32)
+        nc.vector.tensor_copy(out=bias_pos[:], in_=bias_t[:, :, 0])
+        bias_neg = const.tile([P, LOW_TILES], F32)
+        nc.vector.tensor_scalar_mul(out=bias_neg[:], in0=bias_pos[:], scalar1=-1.0)
+
+        pairs_of = {}
+        codes_of = {}
+        gates_of = {}
+
+        def transpose_and_quantise(i):
+            x_sb = stream.tile([P, ROWS * FEATURES], BF16)
+            nc.sync.dma_start(out=x_sb[:], in_=x_chunks[i])
+            x_words = x_sb[:].bitcast(F32).rearrange("p (r w j) -> p r w j", r=ROWS, w=WORD_BLOCKS)
+            pairs = stream.tile([P, WORD_BLOCKS * CHUNK * 2], BF16)
+            pairs_blocks = pairs[:].rearrange("p (w n) -> p w n", w=WORD_BLOCKS)
+            for w in range(WORD_BLOCKS):
+                xt = ps_x.tile([P, CHUNK], F32)
+                for r in range(ROWS):
+                    nc.tensor.transpose(xt[:, r * P : (r + 1) * P], x_words[:, r, w, :], ident[:])
+                nc.scalar.copy(out=pairs_blocks[:, w, :], in_=xt[:].bitcast(BF16))
+            pairs_words = pairs[:].bitcast(F32).rearrange("p (g u b) -> p g u b", g=PASSES, u=2)
+            grouped = work.tile([P, PASSES * CHUNK * 4], BF16, align_bytes=64)
+            grouped_words = grouped[:].bitcast(F32).rearrange("p (g b u) -> p g b u", g=PASSES, u=2)
+            x_codes = stream.tile([P, PASSES, CHUNK], U32, align_bytes=64)
+            x_scales = stream.tile([P, PASSES, CHUNK], U8, align_bytes=64)
+            for g in range(PASSES):
+                nc.vector.tensor_copy(out=grouped_words[:, g], in_=pairs_words[:, g].rearrange("p u b -> p b u"))
+            grouped_passes = grouped[:].rearrange("p (g n) -> p g n", g=PASSES)
+            for g in range(PASSES):
+                nc.vector.quantize_mx(
+                    out=x_codes[:, g, :].bitcast(FP8X4), scales=x_scales[:, g, :], in_=grouped_passes[:, g, :]
+                )
+            pairs_of[i] = pairs
+            codes_of[i] = (x_codes, x_scales)
+
+        def gates_and_top_tree(i):
+            pairs_view = pairs_of[i][:].rearrange("p (w b e) -> p w b e", w=WORD_BLOCKS, e=2)
+            x_codes, x_scales = codes_of[i]
+            z_top = ps_top.tile([P, ROWS, TOP], F32)
+            for r in range(ROWS):
+                nc.tensor.matmul(out=z_top[:, r, :], lhsT=ones[:], rhs=bias_row[:, 0:TOP], start=True, stop=False)
+                for w in range(WORD_BLOCKS):
+                    for e in range(2):
+                        nc.tensor.matmul(
+                            out=z_top[:, r, :],
+                            lhsT=pairs_view[:, w, r * P : (r + 1) * P, e],
+                            rhs=w_top[:, w, e, :],
+                            start=False,
+                            stop=(w == WORD_BLOCKS - 1 and e == 1),
+                        )
+            go_top = work.tile([P, 2, ROWS, TOP], F32)
+            nc.scalar.activation(out=go_top[:, 1], in_=z_top[:], func=SIGMOID)
+            nc.scalar.activation(out=go_top[:, 0], in_=z_top[:], func=SIGMOID, scale=-1.0)
+
+            right7 = stream.tile([P, CHUNK], F32)
+            go8 = stream.tile([P, 4, CHUNK], F32)
+            for nt in range(LOW_TILES):
+                z_low = ps_low.tile([P, CHUNK], F32)
+                for g in range(PASSES):
+                    nc.tensor.matmul_mx(
+                        out=z_low[:],
+                        lhsT=w_codes[:, g, nt, :].bitcast(FP8X4),
+                        lhsT_scale=w_scales[:, g, nt, :],
+                        rhs=x_codes[:, g, :].bitcast(FP8X4),
+                        rhs_scale=x_scales[:, g, :],
+                        start=(g == 0),
+                        stop=(g == PASSES - 1),
+                    )
+                if nt == 0:
+                    nc.scalar.activation(out=right7[:], in_=z_low[:], func=SIGMOID, bias=bias_pos[:, 0:1])
+                else:
+                    c1 = nt - 1
+                    nc.scalar.activation(
+                        out=go8[:, 2 * c1 + 1, :], in_=z_low[:], func=SIGMOID, bias=bias_pos[:, nt : nt + 1]
+                    )
+                    nc.scalar.activation(
+                        out=go8[:, 2 * c1, :], in_=z_low[:], func=SIGMOID, bias=bias_neg[:, nt : nt + 1], scale=-1.0
+                    )
+
+            go_view = go_top[:].rearrange("p c r n -> p r n c")
+            reach = go_view[:, :, 0, :]
+            for level in range(1, TOP_LEVELS):
+                n = 2**level
+                children = work.tile([P, ROWS, n, 2], F32, name="reach%d" % (level + 1))
+                nc.vector.tensor_tensor(
+                    out=children[:],
+                    in0=go_view[:, :, n - 1 : 2 * n - 1, :],
+                    in1=reach.unsqueeze(3).to_broadcast([P, ROWS, n, 2]),
+                    op=MULT,
+                )
+                reach = children[:].rearrange("p r j c -> p r (j c)")
+            gates_of[i] = (reach, right7, go8)
+
+        def low_levels_and_leaves(i):
+            reach7, right7, go8 = gates_of[i]
+            reach7_t = ps_p7.tile([P, CHUNK], F32)
+            for r in range(ROWS):
+                nc.tensor.transpose(reach7_t[:, r * P : (r + 1) * P], reach7[:, r, :], ident[:])
+            reach8 = work.tile([P, 2, CHUNK], F32)
+            nc.vector.tensor_tensor(out=reach8[:, 1, :], in0=right7[:], in1=reach7_t[:], op=MULT)
+            nc.vector.tensor_tensor(out=reach8[:, 0, :], in0=reach7_t[:], in1=reach8[:, 1, :], op=SUBTRACT)
+            probs = work.tile([P, CHUNK, 2, 2], BF16, align_bytes=64)
+            nc.vector.tensor_tensor(
+                out=probs[:],
+                in0=go8[:].rearrange("p (c1 c2) b -> p b c1 c2", c1=2),
+                in1=reach8[:].rearrange("p c1 b -> p b c1").unsqueeze(3).to_broadcast([P, CHUNK, 2, 2]),
+                op=MULT,
+            )
+            p_codes = work.tile([P, CHUNK], U32, align_bytes=64)
+            p_scales = work.tile([P, CHUNK], U8, align_bytes=64)
+            nc.vector.quantize_mx(
+                out=p_codes[:].bitcast(FP8X4), scales=p_scales[:], in_=probs[:].rearrange("p b c1 c2 -> p (b c1 c2)")
+            )
+            acc = ps_out.tile([P, ROWS, CLASSES], F32)
+            for r in range(ROWS):
+                nc.tensor.matmul_mx(
+                    out=acc[:, r, :],
+                    lhsT=p_codes[:, r * P : (r + 1) * P].bitcast(FP8X4),
+                    lhsT_scale=p_scales[:, r * P : (r + 1) * P],
+                    rhs=leaf_codes[:].bitcast(FP8X4),
+                    rhs_scale=leaf_scales[:],
+                    start=True,
+                    stop=True,
+                )
+            result = work.tile([P, ROWS * CLASSES], F32)
+            nc.scalar.copy(out=result[:], in_=acc[:].rearrange("p r c -> p (r c)"))
+            nc.sync.dma_start(out=out_chunks[i], in_=result[:])
+
+        for step in range(N_CHUNKS + 2):
+            if step < N_CHUNKS:
+                transpose_and_quantise(step)
+            if 0 <= step - 1 < N_CHUNKS:
+                gates_and_top_tree(step - 1)
+            if 0 <= step - 2 < N_CHUNKS:
+                low_levels_and_leaves(step - 2)

@@ -34,53 +34,28 @@ def tile_treemodel_t_kernel(tc, x, w_gate, b_gate, leaf_logits, out):
     out_chunks = out.rearrange("(i p r) c -> i p (r c)", p=P, r=ROWS)
 
     with tc.tile_pool(name="const", bufs=1) as const, tc.tile_pool(name="setup", bufs=1) as setup, tc.tile_pool(
-        name="stream", bufs=3
-    ) as stream, tc.tile_pool(name="work", bufs=2) as work, tc.psum_pool(name="ps_x", bufs=2) as ps_x, tc.psum_pool(
-        name="ps_top", bufs=1
-    ) as ps_top, tc.psum_pool(name="ps_low", bufs=3) as ps_low, tc.psum_pool(name="ps_p7", bufs=1) as ps_p7, tc.psum_pool(
-        name="ps_out", bufs=1
-    ) as ps_out:
+        name="two", bufs=2
+    ) as two, tc.tile_pool(name="three", bufs=3) as three, tc.tile_pool(name="four", bufs=4) as four, tc.psum_pool(
+        name="ps_x", bufs=2
+    ) as ps_x, tc.psum_pool(name="ps_top", bufs=1) as ps_top, tc.psum_pool(name="ps_low", bufs=3) as ps_low, tc.psum_pool(
+        name="ps_p7", bufs=1
+    ) as ps_p7, tc.psum_pool(name="ps_out", bufs=1) as ps_out, tc.manual_schedule():
+
         ident = const.tile([P, P], F32)
         make_identity(nc, ident[:])
         ones = const.tile([P, P], BF16)
         nc.vector.memset(ones[:], 1.0)
+        warm = const.tile([P, 1], F32)
+        nc.scalar.activation(out=warm[:], in_=ones[:, 0:1], func=SIGMOID)
 
         bias_row = const.tile([P, LEAVES], BF16)
         nc.vector.memset(bias_row[:], 0.0)
         nc.sync.dma_start(out=bias_row[0:1, 0:NODES], in_=b_gate.unsqueeze(0))
-
         w_sb = setup.tile([P, WORD_BLOCKS, 2 * NODES], BF16)
         nc.sync.dma_start(out=w_sb[:], in_=w_gate.rearrange("(w p e) n -> p w (e n)", w=WORD_BLOCKS, p=P, e=2))
         w_view = w_sb[:].rearrange("p w (e n) -> p w e n", e=2)
         leaf_sb = setup.tile([P, 4, CLASSES], BF16)
         nc.sync.dma_start(out=leaf_sb[:], in_=leaf_logits.rearrange("(p t) c -> p t c", t=4))
-
-        w_top = const.tile([P, WORD_BLOCKS, 2, TOP], BF16)
-        nc.vector.tensor_copy(out=w_top[:], in_=w_view[:, :, :, 0:TOP])
-
-        w_grouped = setup.tile([P, PASSES, LOW_TILES, 4 * P], BF16, align_bytes=64)
-        w_codes = const.tile([P, PASSES, LOW_TILES, P], U32, align_bytes=64)
-        w_scales = const.tile([P, PASSES, LOW_TILES, P], U8, align_bytes=64)
-        low_columns = [slice(127, 255), slice(255, 511, 2), slice(256, 511, 2)]
-        for g in range(PASSES):
-            for nt in range(LOW_TILES):
-                nc.vector.tensor_copy(
-                    out=w_grouped[:, g, nt, :].rearrange("p (m u e) -> p m u e", u=2, e=2),
-                    in_=w_view[:, 2 * g : 2 * g + 2, :, low_columns[nt]].rearrange("p u e m -> p m u e"),
-                )
-        for g in range(PASSES):
-            for nt in range(LOW_TILES):
-                nc.vector.quantize_mx(
-                    out=w_codes[:, g, nt, :].bitcast(FP8X4), scales=w_scales[:, g, nt, :], in_=w_grouped[:, g, nt, :]
-                )
-
-        leaf_grouped = setup.tile([P, CLASSES, 4], BF16, align_bytes=64)
-        nc.vector.tensor_copy(out=leaf_grouped[:], in_=leaf_sb[:].rearrange("p t c -> p c t"))
-        leaf_codes = const.tile([P, CLASSES], U32, align_bytes=64)
-        leaf_scales = const.tile([P, CLASSES], U8, align_bytes=64)
-        nc.vector.quantize_mx(
-            out=leaf_codes[:].bitcast(FP8X4), scales=leaf_scales[:], in_=leaf_grouped[:].rearrange("p c t -> p (c t)")
-        )
 
         bias_sel = setup.tile([P, LOW_TILES, P], F32)
         nc.vector.tensor_copy(out=bias_sel[:, 0, :], in_=bias_row[:, 127:255])
@@ -91,43 +66,97 @@ def tile_treemodel_t_kernel(tc, x, w_gate, b_gate, leaf_logits, out):
         bias_pos = const.tile([P, LOW_TILES], F32)
         nc.vector.tensor_copy(out=bias_pos[:], in_=bias_t[:, :, 0])
         bias_neg = const.tile([P, LOW_TILES], F32)
-        nc.vector.tensor_scalar_mul(out=bias_neg[:], in0=bias_pos[:], scalar1=-1.0)
+        nc.vector.tensor_scalar_mul(out=bias_neg[:], in0=bias_t[:, :, 0], scalar1=-1.0)
 
+        w_top = const.tile([P, WORD_BLOCKS, 2, TOP], BF16)
+        nc.vector.tensor_copy(out=w_top[:], in_=w_view[:, :, :, 0:TOP])
+        w_grouped = setup.tile([P, PASSES, LOW_TILES, 4 * P], BF16, align_bytes=64)
+        w_codes = const.tile([P, PASSES, LOW_TILES, P], U32, align_bytes=64)
+        w_scales = const.tile([P, PASSES, LOW_TILES, P], U8, align_bytes=64)
+        low_columns = [slice(127, 255), slice(255, 511, 2), slice(256, 511, 2)]
+        for g in range(PASSES):
+            for nt in range(LOW_TILES):
+                nc.vector.tensor_copy(
+                    out=w_grouped[:, g, nt, :].rearrange("p (m u e) -> p m u e", u=2, e=2),
+                    in_=w_view[:, 2 * g : 2 * g + 2, :, low_columns[nt]].rearrange("p u e m -> p m u e"),
+                )
+        leaf_grouped = setup.tile([P, CLASSES, 4], BF16, align_bytes=64)
+        nc.vector.tensor_copy(out=leaf_grouped[:], in_=leaf_sb[:].rearrange("p t c -> p c t"))
+        for g in range(PASSES):
+            for nt in range(LOW_TILES):
+                nc.vector.quantize_mx(
+                    out=w_codes[:, g, nt, :].bitcast(FP8X4), scales=w_scales[:, g, nt, :], in_=w_grouped[:, g, nt, :]
+                )
+        leaf_codes = const.tile([P, CLASSES], U32, align_bytes=64)
+        leaf_scales = const.tile([P, CLASSES], U8, align_bytes=64)
+        nc.vector.quantize_mx(
+            out=leaf_codes[:].bitcast(FP8X4), scales=leaf_scales[:], in_=leaf_grouped[:].rearrange("p c t -> p (c t)")
+        )
+
+        x_of = {}
         pairs_of = {}
+        grouped_of = {}
         codes_of = {}
-        gates_of = {}
+        z_top_of = {}
+        go_top_of = {}
+        reach_of = {}
+        low_of = {}
+        reach7_t_of = {}
+        reach8_of = {}
+        probs_of = {}
+        p_codes_of = {}
 
-        def transpose_and_quantise(i):
-            x_sb = stream.tile([P, ROWS * FEATURES], BF16)
-            nc.sync.dma_start(out=x_sb[:], in_=x_chunks[i])
-            x_words = x_sb[:].bitcast(F32).rearrange("p (r w j) -> p r w j", r=ROWS, w=WORD_BLOCKS)
-            pairs = stream.tile([P, WORD_BLOCKS * CHUNK * 2], BF16)
-            pairs_blocks = pairs[:].rearrange("p (w n) -> p w n", w=WORD_BLOCKS)
-            for w in range(WORD_BLOCKS):
+        def live(c):
+            return 0 <= c < N_CHUNKS
+
+        def load_x(c):
+            if not live(c):
+                return
+            x_sb = three.tile([P, ROWS * FEATURES], BF16)
+            nc.sync.dma_start(out=x_sb[:], in_=x_chunks[c])
+            x_of[c] = x_sb
+
+        def transpose_x(c, blocks):
+            if not live(c):
+                return
+            if blocks[0] == 0:
+                pairs = three.tile([P, WORD_BLOCKS * CHUNK * 2], BF16)
+                pairs_of[c] = pairs
+            x_words = x_of[c][:].bitcast(F32).rearrange("p (r w j) -> p r w j", r=ROWS, w=WORD_BLOCKS)
+            pairs_words = pairs_of[c][:].bitcast(F32).rearrange("p (w b) -> p w b", w=WORD_BLOCKS)
+            for w in blocks:
                 xt = ps_x.tile([P, CHUNK], F32)
                 for r in range(ROWS):
                     nc.tensor.transpose(xt[:, r * P : (r + 1) * P], x_words[:, r, w, :], ident[:])
-                nc.scalar.copy(out=pairs_blocks[:, w, :], in_=xt[:].bitcast(BF16))
-            pairs_words = pairs[:].bitcast(F32).rearrange("p (g u b) -> p g u b", g=PASSES, u=2)
-            grouped = work.tile([P, PASSES * CHUNK * 4], BF16, align_bytes=64)
-            grouped_words = grouped[:].bitcast(F32).rearrange("p (g b u) -> p g b u", g=PASSES, u=2)
-            x_codes = stream.tile([P, PASSES, CHUNK], U32, align_bytes=64)
-            x_scales = stream.tile([P, PASSES, CHUNK], U8, align_bytes=64)
-            for g in range(PASSES):
-                nc.vector.tensor_copy(out=grouped_words[:, g], in_=pairs_words[:, g].rearrange("p u b -> p b u"))
-            grouped_passes = grouped[:].rearrange("p (g n) -> p g n", g=PASSES)
-            for g in range(PASSES):
-                nc.vector.quantize_mx(
-                    out=x_codes[:, g, :].bitcast(FP8X4), scales=x_scales[:, g, :], in_=grouped_passes[:, g, :]
-                )
-            pairs_of[i] = pairs
-            codes_of[i] = (x_codes, x_scales)
+                nc.scalar.copy(out=pairs_words[:, w, :], in_=xt[:])
 
-        def gates_and_top_tree(i):
-            pairs_view = pairs_of[i][:].rearrange("p (w b e) -> p w b e", w=WORD_BLOCKS, e=2)
-            x_codes, x_scales = codes_of[i]
-            z_top = ps_top.tile([P, ROWS, TOP], F32)
-            for r in range(ROWS):
+        def regroup_x(c):
+            if not live(c):
+                return
+            grouped = two.tile([P, PASSES * CHUNK * 4], BF16, align_bytes=64)
+            nc.vector.tensor_copy(
+                out=grouped[:].bitcast(F32).rearrange("p (g b u) -> p g b u", g=PASSES, u=2),
+                in_=pairs_of[c][:].bitcast(F32).rearrange("p (g u b) -> p g b u", g=PASSES, u=2),
+            )
+            grouped_of[c] = grouped
+
+        def quantise_x(c):
+            if not live(c):
+                return
+            x_codes = three.tile([P, PASSES * CHUNK], U32, align_bytes=64)
+            x_scales = three.tile([P, PASSES * CHUNK], U8, align_bytes=64)
+            nc.vector.quantize_mx(out=x_codes[:].bitcast(FP8X4), scales=x_scales[:], in_=grouped_of[c][:])
+            codes_of[c] = (x_codes, x_scales)
+
+        def top_gates(c, rows):
+            if not live(c):
+                return
+            if rows[0] == 0:
+                z_top = ps_top.tile([P, ROWS, TOP], F32)
+                z_top_of[c] = z_top
+            z_top = z_top_of[c]
+            pairs_view = pairs_of[c][:].rearrange("p (w b e) -> p w b e", w=WORD_BLOCKS, e=2)
+            for r in rows:
                 nc.tensor.matmul(out=z_top[:, r, :], lhsT=ones[:], rhs=bias_row[:, 0:TOP], start=True, stop=False)
                 for w in range(WORD_BLOCKS):
                     for e in range(2):
@@ -138,12 +167,18 @@ def tile_treemodel_t_kernel(tc, x, w_gate, b_gate, leaf_logits, out):
                             start=False,
                             stop=(w == WORD_BLOCKS - 1 and e == 1),
                         )
-            go_top = work.tile([P, 2, ROWS, TOP], F32)
-            nc.scalar.activation(out=go_top[:, 1], in_=z_top[:], func=SIGMOID)
-            nc.scalar.activation(out=go_top[:, 0], in_=z_top[:], func=SIGMOID, scale=-1.0)
+            if rows[-1] == ROWS - 1:
+                go_top = three.tile([P, 2, ROWS, TOP], F32)
+                nc.scalar.activation(out=go_top[:, 1], in_=z_top[:], func=SIGMOID)
+                nc.scalar.activation(out=go_top[:, 0], in_=z_top[:], func=SIGMOID, scale=-1.0)
+                go_top_of[c] = go_top
 
-            right7 = stream.tile([P, CHUNK], F32)
-            go8 = stream.tile([P, 4, CHUNK], F32)
+        def low_gates(c):
+            if not live(c):
+                return
+            x_codes, x_scales = codes_of[c]
+            right7 = four.tile([P, CHUNK], F32)
+            go8 = four.tile([P, 4, CHUNK], F32)
             for nt in range(LOW_TILES):
                 z_low = ps_low.tile([P, CHUNK], F32)
                 for g in range(PASSES):
@@ -151,8 +186,8 @@ def tile_treemodel_t_kernel(tc, x, w_gate, b_gate, leaf_logits, out):
                         out=z_low[:],
                         lhsT=w_codes[:, g, nt, :].bitcast(FP8X4),
                         lhsT_scale=w_scales[:, g, nt, :],
-                        rhs=x_codes[:, g, :].bitcast(FP8X4),
-                        rhs_scale=x_scales[:, g, :],
+                        rhs=x_codes[:, g * CHUNK : (g + 1) * CHUNK].bitcast(FP8X4),
+                        rhs_scale=x_scales[:, g * CHUNK : (g + 1) * CHUNK],
                         start=(g == 0),
                         stop=(g == PASSES - 1),
                     )
@@ -166,41 +201,73 @@ def tile_treemodel_t_kernel(tc, x, w_gate, b_gate, leaf_logits, out):
                     nc.scalar.activation(
                         out=go8[:, 2 * c1, :], in_=z_low[:], func=SIGMOID, bias=bias_neg[:, nt : nt + 1], scale=-1.0
                     )
+            low_of[c] = (right7, go8)
 
-            go_view = go_top[:].rearrange("p c r n -> p r n c")
-            reach = go_view[:, :, 0, :]
-            for level in range(1, TOP_LEVELS):
-                n = 2**level
-                children = work.tile([P, ROWS, n, 2], F32, name="reach%d" % (level + 1))
-                nc.vector.tensor_tensor(
-                    out=children[:],
-                    in0=go_view[:, :, n - 1 : 2 * n - 1, :],
-                    in1=reach.unsqueeze(3).to_broadcast([P, ROWS, n, 2]),
-                    op=MULT,
-                )
-                reach = children[:].rearrange("p r j c -> p r (j c)")
-            gates_of[i] = (reach, right7, go8)
-
-        def low_levels_and_leaves(i):
-            reach7, right7, go8 = gates_of[i]
-            reach7_t = ps_p7.tile([P, CHUNK], F32)
-            for r in range(ROWS):
-                nc.tensor.transpose(reach7_t[:, r * P : (r + 1) * P], reach7[:, r, :], ident[:])
-            reach8 = work.tile([P, 2, CHUNK], F32)
-            nc.vector.tensor_tensor(out=reach8[:, 1, :], in0=right7[:], in1=reach7_t[:], op=MULT)
-            nc.vector.tensor_tensor(out=reach8[:, 0, :], in0=reach7_t[:], in1=reach8[:, 1, :], op=SUBTRACT)
-            probs = work.tile([P, CHUNK, 2, 2], BF16, align_bytes=64)
+        def tree_level(c, level):
+            if not live(c):
+                return
+            go_view = go_top_of[c][:].rearrange("p c r n -> p r n c")
+            if level == 1:
+                reach_of[c] = go_view[:, :, 0, :]
+            n = 2**level
+            children = three.tile([P, ROWS, n, 2], F32, name="reach%d" % (level + 1))
             nc.vector.tensor_tensor(
-                out=probs[:],
-                in0=go8[:].rearrange("p (c1 c2) b -> p b c1 c2", c1=2),
-                in1=reach8[:].rearrange("p c1 b -> p b c1").unsqueeze(3).to_broadcast([P, CHUNK, 2, 2]),
+                out=children[:],
+                in0=go_view[:, :, n - 1 : 2 * n - 1, :],
+                in1=reach_of[c].unsqueeze(3).to_broadcast([P, ROWS, n, 2]),
                 op=MULT,
             )
-            p_codes = work.tile([P, CHUNK], U32, align_bytes=64)
-            p_scales = work.tile([P, CHUNK], U8, align_bytes=64)
-            nc.vector.quantize_mx(
-                out=p_codes[:].bitcast(FP8X4), scales=p_scales[:], in_=probs[:].rearrange("p b c1 c2 -> p (b c1 c2)")
+            reach_of[c] = children[:].rearrange("p r j c -> p r (j c)")
+
+        def transpose_reach7(c):
+            if not live(c):
+                return
+            reach7_t = ps_p7.tile([P, CHUNK], F32)
+            for r in range(ROWS):
+                nc.tensor.transpose(reach7_t[:, r * P : (r + 1) * P], reach_of[c][:, r, :], ident[:])
+            reach7_t_of[c] = reach7_t
+
+        def level7_right(c):
+            if not live(c):
+                return
+            reach8 = two.tile([P, 2, CHUNK], F32)
+            nc.vector.tensor_tensor(out=reach8[:, 1, :], in0=low_of[c][0][:], in1=reach7_t_of[c][:], op=MULT)
+            reach8_of[c] = reach8
+
+        def level7_left(c):
+            if not live(c):
+                return
+            reach8 = reach8_of[c]
+            nc.vector.tensor_tensor(out=reach8[:, 0, :], in0=reach7_t_of[c][:], in1=reach8[:, 1, :], op=SUBTRACT)
+
+        def level8(c):
+            if not live(c):
+                return
+            probs = two.tile([P, CHUNK, 2, 2], BF16, align_bytes=64)
+            nc.vector.tensor_tensor(
+                out=probs[:],
+                in0=low_of[c][1][:].rearrange("p (c1 c2) b -> p b c1 c2", c1=2),
+                in1=reach8_of[c][:].rearrange("p c1 b -> p b c1").unsqueeze(3).to_broadcast([P, CHUNK, 2, 2]),
+                op=MULT,
             )
+            probs_of[c] = probs
+
+        def quantise_probs(c):
+            if not live(c):
+                return
+            p_codes = three.tile([P, CHUNK], U32, align_bytes=64)
+            p_scales = three.tile([P, CHUNK], U8, align_bytes=64)
+            nc.vector.quantize_mx(
+                out=p_codes[:].bitcast(FP8X4),
+                scales=p_scales[:],
+                in_=probs_of[c][:].rearrange("p b c1 c2 -> p (b c1 c2)"),
+            )
+            p_codes_of[c] = (p_codes, p_scales)
+
+        def leaves(c):
+            if not live(c):
+                return
+            p_codes, p_scales = p_codes_of[c]
             acc = ps_out.tile([P, ROWS, CLASSES], F32)
             for r in range(ROWS):
                 nc.tensor.matmul_mx(
@@ -212,14 +279,28 @@ def tile_treemodel_t_kernel(tc, x, w_gate, b_gate, leaf_logits, out):
                     start=True,
                     stop=True,
                 )
-            result = work.tile([P, ROWS * CLASSES], F32)
+            result = three.tile([P, ROWS * CLASSES], F32)
             nc.scalar.copy(out=result[:], in_=acc[:].rearrange("p r c -> p (r c)"))
-            nc.sync.dma_start(out=out_chunks[i], in_=result[:])
+            nc.sync.dma_start(out=out_chunks[c], in_=result[:])
 
-        for step in range(N_CHUNKS + 2):
-            if step < N_CHUNKS:
-                transpose_and_quantise(step)
-            if 0 <= step - 1 < N_CHUNKS:
-                gates_and_top_tree(step - 1)
-            if 0 <= step - 2 < N_CHUNKS:
-                low_levels_and_leaves(step - 2)
+        for j in range(-3, N_CHUNKS + 3):
+            load_x(j + 3)
+            transpose_x(j + 2, [0, 1])
+            top_gates(j, [0, 1])
+            transpose_x(j + 2, [2, 3])
+            transpose_reach7(j - 2)
+            top_gates(j, [2, 3])
+            low_gates(j)
+            regroup_x(j + 1)
+            tree_level(j - 1, 1)
+            quantise_probs(j - 3)
+            tree_level(j - 1, 2)
+            quantise_x(j + 1)
+            tree_level(j - 1, 3)
+            level7_right(j - 2)
+            tree_level(j - 1, 4)
+            level7_left(j - 2)
+            tree_level(j - 1, 5)
+            level8(j - 2)
+            tree_level(j - 1, 6)
+            leaves(j - 3)

@@ -36,10 +36,8 @@ def tile_treemodel_t_kernel(tc, x, w_gate, b_gate, leaf_logits, out):
     with tc.tile_pool(name="const", bufs=1) as const, tc.tile_pool(name="setup", bufs=1) as setup, tc.tile_pool(
         name="two", bufs=2
     ) as two, tc.tile_pool(name="three", bufs=3) as three, tc.tile_pool(name="four", bufs=4) as four, tc.psum_pool(
-        name="ps_x", bufs=2
-    ) as ps_x, tc.psum_pool(name="ps_top", bufs=1) as ps_top, tc.psum_pool(name="ps_low", bufs=3) as ps_low, tc.psum_pool(
-        name="ps_p7", bufs=1
-    ) as ps_p7, tc.psum_pool(name="ps_out", bufs=1) as ps_out, tc.manual_schedule():
+        name="psum", bufs=8
+    ) as psum, tc.manual_schedule():
 
         ident = const.tile([P, P], F32)
         make_identity(nc, ident[:])
@@ -60,7 +58,7 @@ def tile_treemodel_t_kernel(tc, x, w_gate, b_gate, leaf_logits, out):
         bias_sel = setup.tile([P, LOW_TILES, P], F32)
         nc.vector.tensor_copy(out=bias_sel[:, 0, :], in_=bias_row[:, 127:255])
         nc.vector.tensor_copy(out=bias_sel[:, 1:3, :], in_=bias_row[:, 255:511].rearrange("p (m c) -> p c m", c=2))
-        bias_t = ps_low.tile([P, LOW_TILES, P], F32, tag="z_low")
+        bias_t = psum.tile([P, LOW_TILES, P], F32, tag="bank")
         for nt in range(LOW_TILES):
             nc.tensor.transpose(bias_t[:, nt, :], bias_sel[:, nt, :], ident[:])
         bias_pos = const.tile([P, LOW_TILES], F32)
@@ -125,7 +123,7 @@ def tile_treemodel_t_kernel(tc, x, w_gate, b_gate, leaf_logits, out):
             x_words = x_of[c][:].bitcast(F32).rearrange("p (r w j) -> p r w j", r=ROWS, w=WORD_BLOCKS)
             pairs_words = pairs_of[c][:].bitcast(F32).rearrange("p (w b) -> p w b", w=WORD_BLOCKS)
             for w in blocks:
-                xt = ps_x.tile([P, CHUNK], F32)
+                xt = psum.tile([P, CHUNK], F32, tag="bank")
                 for r in range(ROWS):
                     nc.tensor.transpose(xt[:, r * P : (r + 1) * P], x_words[:, r, w, :], ident[:])
                 nc.scalar.copy(out=pairs_words[:, w, :], in_=xt[:])
@@ -152,7 +150,7 @@ def tile_treemodel_t_kernel(tc, x, w_gate, b_gate, leaf_logits, out):
             if not live(c):
                 return
             if rows[0] == 0:
-                z_top = ps_top.tile([P, ROWS, TOP], F32)
+                z_top = psum.tile([P, ROWS, TOP], F32, tag="bank")
                 z_top_of[c] = z_top
             z_top = z_top_of[c]
             pairs_view = pairs_of[c][:].rearrange("p (w b e) -> p w b e", w=WORD_BLOCKS, e=2)
@@ -180,7 +178,7 @@ def tile_treemodel_t_kernel(tc, x, w_gate, b_gate, leaf_logits, out):
             right7 = four.tile([P, CHUNK], F32)
             go8 = four.tile([P, 4, CHUNK], F32)
             for nt in range(LOW_TILES):
-                z_low = ps_low.tile([P, CHUNK], F32)
+                z_low = psum.tile([P, CHUNK], F32, tag="bank")
                 for g in range(PASSES):
                     nc.tensor.matmul_mx(
                         out=z_low[:],
@@ -222,7 +220,7 @@ def tile_treemodel_t_kernel(tc, x, w_gate, b_gate, leaf_logits, out):
         def transpose_reach7(c):
             if not live(c):
                 return
-            reach7_t = ps_p7.tile([P, CHUNK], F32)
+            reach7_t = psum.tile([P, CHUNK], F32, tag="bank")
             for r in range(ROWS):
                 nc.tensor.transpose(reach7_t[:, r * P : (r + 1) * P], reach_of[c][:, r, :], ident[:])
             reach7_t_of[c] = reach7_t
@@ -268,7 +266,7 @@ def tile_treemodel_t_kernel(tc, x, w_gate, b_gate, leaf_logits, out):
             if not live(c):
                 return
             p_codes, p_scales = p_codes_of[c]
-            acc = ps_out.tile([P, ROWS, CLASSES], F32)
+            acc = psum.tile([P, ROWS, CLASSES], F32, tag="bank")
             for r in range(ROWS):
                 nc.tensor.matmul_mx(
                     out=acc[:, r, :],

@@ -39,6 +39,18 @@ def tile_treemodel_t_kernel(tc, x, w_gate, b_gate, leaf_logits, out):
         name="psum", bufs=8
     ) as psum, tc.manual_schedule():
 
+        x_of = {}
+
+        def live(c):
+            return 0 <= c < N_CHUNKS
+
+        def load_x(c):
+            if not live(c):
+                return
+            x_sb = three.tile([P, ROWS * FEATURES], BF16)
+            nc.sync.dma_start(out=x_sb[:], in_=x_chunks[c])
+            x_of[c] = x_sb
+
         ident = const.tile([P, P], F32)
         make_identity(nc, ident[:])
         ones = const.tile([P, P], BF16)
@@ -49,6 +61,7 @@ def tile_treemodel_t_kernel(tc, x, w_gate, b_gate, leaf_logits, out):
         bias_row = const.tile([P, LEAVES], BF16)
         nc.vector.memset(bias_row[:], 0.0)
         nc.sync.dma_start(out=bias_row[0:1, 0:NODES], in_=b_gate.unsqueeze(0))
+        load_x(0)
         w_sb = setup.tile([P, WORD_BLOCKS, 2 * NODES], BF16)
         nc.sync.dma_start(out=w_sb[:], in_=w_gate.rearrange("(w p e) n -> p w (e n)", w=WORD_BLOCKS, p=P, e=2))
         w_view = w_sb[:].rearrange("p w (e n) -> p w e n", e=2)
@@ -91,7 +104,6 @@ def tile_treemodel_t_kernel(tc, x, w_gate, b_gate, leaf_logits, out):
             out=leaf_codes[:].bitcast(FP8X4), scales=leaf_scales[:], in_=leaf_grouped[:].rearrange("p c t -> p (c t)")
         )
 
-        x_of = {}
         pairs_of = {}
         grouped_of = {}
         codes_of = {}
@@ -103,16 +115,6 @@ def tile_treemodel_t_kernel(tc, x, w_gate, b_gate, leaf_logits, out):
         reach8_of = {}
         probs_of = {}
         p_codes_of = {}
-
-        def live(c):
-            return 0 <= c < N_CHUNKS
-
-        def load_x(c):
-            if not live(c):
-                return
-            x_sb = three.tile([P, ROWS * FEATURES], BF16)
-            nc.sync.dma_start(out=x_sb[:], in_=x_chunks[c])
-            x_of[c] = x_sb
 
         def transpose_x(c, blocks):
             if not live(c):
@@ -281,7 +283,7 @@ def tile_treemodel_t_kernel(tc, x, w_gate, b_gate, leaf_logits, out):
             nc.scalar.copy(out=result[:], in_=acc[:].rearrange("p r c -> p (r c)"))
             nc.sync.dma_start(out=out_chunks[c], in_=result[:])
 
-        for j in range(-3, N_CHUNKS + 3):
+        for j in range(-2, N_CHUNKS + 3):
             load_x(j + 3)
             transpose_x(j + 2, [0, 1])
             top_gates(j, [0, 1])
@@ -289,16 +291,16 @@ def tile_treemodel_t_kernel(tc, x, w_gate, b_gate, leaf_logits, out):
             transpose_reach7(j - 2)
             top_gates(j, [2, 3])
             low_gates(j)
-            regroup_x(j + 1)
             tree_level(j - 1, 1)
-            quantise_probs(j - 3)
+            regroup_x(j + 1)
             tree_level(j - 1, 2)
-            quantise_x(j + 1)
+            quantise_probs(j - 3)
             tree_level(j - 1, 3)
-            level7_right(j - 2)
+            quantise_x(j + 1)
             tree_level(j - 1, 4)
-            level7_left(j - 2)
+            level7_right(j - 2)
             tree_level(j - 1, 5)
-            level8(j - 2)
+            level7_left(j - 2)
             tree_level(j - 1, 6)
+            level8(j - 2)
             leaves(j - 3)

@@ -17,7 +17,6 @@ NODES = 511
 LEAVES = 512
 CLASSES = 128
 TOP = 128
-TOP_LEVELS = 7
 ROWS = 4
 CHUNK = P * ROWS
 N_CHUNKS = BATCH // CHUNK
@@ -104,7 +103,6 @@ def tile_treemodel_t_kernel(tc, x, w_gate, b_gate, leaf_logits, out):
             out=leaf_codes[:].bitcast(FP8X4), scales=leaf_scales[:], in_=leaf_grouped[:].rearrange("p c t -> p (c t)")
         )
 
-        pairs_of = {}
         grouped_of = {}
         codes_of = {}
         z_top_of = {}
@@ -116,29 +114,23 @@ def tile_treemodel_t_kernel(tc, x, w_gate, b_gate, leaf_logits, out):
         probs_of = {}
         p_codes_of = {}
 
-        def transpose_x(c, blocks):
+        def transpose_x(c, quarters):
             if not live(c):
                 return
-            if blocks[0] == 0:
-                pairs = three.tile([P, WORD_BLOCKS * CHUNK * 2], BF16)
-                pairs_of[c] = pairs
+            if quarters[0] == 0:
+                grouped = three.tile([P, PASSES * CHUNK * 4], BF16, align_bytes=64)
+                grouped_of[c] = grouped
             x_words = x_of[c][:].bitcast(F32).rearrange("p (r w j) -> p r w j", r=ROWS, w=WORD_BLOCKS)
-            pairs_words = pairs_of[c][:].bitcast(F32).rearrange("p (w b) -> p w b", w=WORD_BLOCKS)
-            for w in blocks:
-                xt = psum.tile([P, CHUNK], F32, tag="bank")
-                for r in range(ROWS):
-                    nc.tensor.transpose(xt[:, r * P : (r + 1) * P], x_words[:, r, w, :], ident[:])
-                nc.scalar.copy(out=pairs_words[:, w, :], in_=xt[:])
-
-        def regroup_x(c):
-            if not live(c):
-                return
-            grouped = two.tile([P, PASSES * CHUNK * 4], BF16, align_bytes=64)
-            nc.vector.tensor_copy(
-                out=grouped[:].bitcast(F32).rearrange("p (g b u) -> p g b u", g=PASSES, u=2),
-                in_=pairs_of[c][:].bitcast(F32).rearrange("p (g u b) -> p g b u", g=PASSES, u=2),
-            )
-            grouped_of[c] = grouped
+            grouped_words = grouped_of[c][:].bitcast(F32).rearrange("p (g h b u) -> p g h b u", g=PASSES, h=2, u=2)
+            for q in quarters:
+                g, h = q // 2, q % 2
+                xt = psum.tile([P, 2, CHUNK // 2], F32, tag="bank")
+                for u in range(2):
+                    for r in range(2):
+                        nc.tensor.transpose(
+                            xt[:, u, r * P : (r + 1) * P], x_words[:, 2 * h + r, 2 * g + u, :], ident[:]
+                        )
+                nc.scalar.copy(out=grouped_words[:, g, h], in_=xt[:].rearrange("p u b -> p b u"))
 
         def quantise_x(c):
             if not live(c):
@@ -155,14 +147,14 @@ def tile_treemodel_t_kernel(tc, x, w_gate, b_gate, leaf_logits, out):
                 z_top = psum.tile([P, ROWS, TOP], F32, tag="bank")
                 z_top_of[c] = z_top
             z_top = z_top_of[c]
-            pairs_view = pairs_of[c][:].rearrange("p (w b e) -> p w b e", w=WORD_BLOCKS, e=2)
+            grouped_view = grouped_of[c][:].rearrange("p (g b u e) -> p g u b e", g=PASSES, u=2, e=2)
             for r in rows:
                 nc.tensor.matmul(out=z_top[:, r, :], lhsT=ones[:], rhs=bias_row[:, 0:TOP], start=True, stop=False)
                 for w in range(WORD_BLOCKS):
                     for e in range(2):
                         nc.tensor.matmul(
                             out=z_top[:, r, :],
-                            lhsT=pairs_view[:, w, r * P : (r + 1) * P, e],
+                            lhsT=grouped_view[:, w // 2, w % 2, r * P : (r + 1) * P, e],
                             rhs=w_top[:, w, e, :],
                             start=False,
                             stop=(w == WORD_BLOCKS - 1 and e == 1),
@@ -240,17 +232,20 @@ def tile_treemodel_t_kernel(tc, x, w_gate, b_gate, leaf_logits, out):
             reach8 = reach8_of[c]
             nc.vector.tensor_tensor(out=reach8[:, 0, :], in0=reach7_t_of[c][:], in1=reach8[:, 1, :], op=SUBTRACT)
 
-        def level8(c):
+        def level8(c, h):
             if not live(c):
                 return
-            probs = two.tile([P, CHUNK, 2, 2], BF16, align_bytes=64)
+            if h == 0:
+                probs = two.tile([P, CHUNK, 2, 2], BF16, align_bytes=64)
+                probs_of[c] = probs
+            half = CHUNK // 2
+            rows = slice(h * half, (h + 1) * half)
             nc.vector.tensor_tensor(
-                out=probs[:],
-                in0=low_of[c][1][:].rearrange("p (c1 c2) b -> p b c1 c2", c1=2),
-                in1=reach8_of[c][:].rearrange("p c1 b -> p b c1").unsqueeze(3).to_broadcast([P, CHUNK, 2, 2]),
+                out=probs_of[c][:, rows],
+                in0=low_of[c][1][:, :, rows].rearrange("p (c1 c2) b -> p b c1 c2", c1=2),
+                in1=reach8_of[c][:, :, rows].rearrange("p c1 b -> p b c1").unsqueeze(3).to_broadcast([P, half, 2, 2]),
                 op=MULT,
             )
-            probs_of[c] = probs
 
         def quantise_probs(c):
             if not live(c):
@@ -292,15 +287,15 @@ def tile_treemodel_t_kernel(tc, x, w_gate, b_gate, leaf_logits, out):
             top_gates(j, [2, 3])
             low_gates(j)
             tree_level(j - 1, 1)
-            regroup_x(j + 1)
-            tree_level(j - 1, 2)
             quantise_probs(j - 3)
-            tree_level(j - 1, 3)
+            tree_level(j - 1, 2)
             quantise_x(j + 1)
-            tree_level(j - 1, 4)
+            tree_level(j - 1, 3)
             level7_right(j - 2)
-            tree_level(j - 1, 5)
+            tree_level(j - 1, 4)
             level7_left(j - 2)
+            tree_level(j - 1, 5)
+            level8(j - 2, 0)
             tree_level(j - 1, 6)
-            level8(j - 2)
+            level8(j - 2, 1)
             leaves(j - 3)

@@ -222,15 +222,25 @@ def tile_treemodel_t_kernel(tc, x, w_gate, b_gate, leaf_logits, out):
         def level7_right(c):
             if not live(c):
                 return
-            reach8 = two.tile([P, 2, CHUNK], F32)
-            nc.vector.tensor_tensor(out=reach8[:, 1, :], in0=low_of[c][0][:], in1=reach7_t_of[c][:], op=MULT)
+            reach8 = two.tile([P, CHUNK // 4, 2, 4], F32)
+            nc.vector.tensor_tensor(
+                out=reach8[:, :, 1, :],
+                in0=low_of[c][0][:].rearrange("p (b i) -> p b i", i=4),
+                in1=reach7_t_of[c][:].rearrange("p (b i) -> p b i", i=4),
+                op=MULT,
+            )
             reach8_of[c] = reach8
 
         def level7_left(c):
             if not live(c):
                 return
             reach8 = reach8_of[c]
-            nc.vector.tensor_tensor(out=reach8[:, 0, :], in0=reach7_t_of[c][:], in1=reach8[:, 1, :], op=SUBTRACT)
+            nc.vector.tensor_tensor(
+                out=reach8[:, :, 0, :],
+                in0=reach7_t_of[c][:].rearrange("p (b i) -> p b i", i=4),
+                in1=reach8[:, :, 1, :],
+                op=SUBTRACT,
+            )
 
         def level8(c, h):
             if not live(c):
@@ -240,10 +250,11 @@ def tile_treemodel_t_kernel(tc, x, w_gate, b_gate, leaf_logits, out):
                 probs_of[c] = probs
             half = CHUNK // 2
             rows = slice(h * half, (h + 1) * half)
+            groups = slice(h * half // 4, (h + 1) * half // 4)
             nc.vector.tensor_tensor(
-                out=probs_of[c][:, rows],
-                in0=low_of[c][1][:, :, rows].rearrange("p (c1 c2) b -> p b c1 c2", c1=2),
-                in1=reach8_of[c][:, :, rows].rearrange("p c1 b -> p b c1").unsqueeze(3).to_broadcast([P, half, 2, 2]),
+                out=probs_of[c][:, rows].rearrange("p (b i) c1 c2 -> p b c1 c2 i", i=4),
+                in0=low_of[c][1][:, :, rows].rearrange("p (c1 c2) (b i) -> p b c1 c2 i", c1=2, i=4),
+                in1=reach8_of[c][:, groups].unsqueeze(3).to_broadcast([P, half // 4, 2, 2, 4]),
                 op=MULT,
             )
 

@@ -47,7 +47,11 @@ def tile_treemodel_t_kernel(tc, x, w_gate, b_gate, leaf_logits, out):
             if not live(c):
                 return
             x_sb = three.tile([P, ROWS * FEATURES], BF16)
-            nc.sync.dma_start(out=x_sb[:], in_=x_chunks[c])
+            parts = 2 if c == 0 else 1
+            width = ROWS * FEATURES // parts
+            for i in range(parts):
+                columns = slice(i * width, (i + 1) * width)
+                nc.sync.dma_start(out=x_sb[:, columns], in_=x_chunks[c][:, columns])
             x_of[c] = x_sb
 
         ident = const.tile([P, P], F32)
@@ -57,51 +61,20 @@ def tile_treemodel_t_kernel(tc, x, w_gate, b_gate, leaf_logits, out):
         warm = const.tile([P, 1], F32)
         nc.scalar.activation(out=warm[:], in_=ones[:, 0:1], func=SIGMOID)
 
+        load_x(0)
         bias_row = const.tile([P, LEAVES], BF16)
         nc.vector.memset(bias_row[:], 0.0)
         nc.sync.dma_start(out=bias_row[0:1, 0:NODES], in_=b_gate.unsqueeze(0))
-        load_x(0)
-        w_sb = setup.tile([P, WORD_BLOCKS, 2 * NODES], BF16)
-        nc.sync.dma_start(out=w_sb[:], in_=w_gate.rearrange("(w p e) n -> p w (e n)", w=WORD_BLOCKS, p=P, e=2))
-        w_view = w_sb[:].rearrange("p w (e n) -> p w e n", e=2)
+        w_hbm = w_gate.rearrange("(w p e) n -> p w (e n)", w=WORD_BLOCKS, p=P, e=2)
+        w_views = []
+        for g in range(PASSES):
+            w_sb = setup.tile([P, 2, 2 * NODES], BF16, name="w_sb%d" % g)
+            nc.sync.dma_start(out=w_sb[:], in_=w_hbm[:, 2 * g : 2 * g + 2])
+            w_views.append(w_sb[:].rearrange("p u (e n) -> p u e n", e=2))
+        load_x(1)
         leaf_sb = setup.tile([P, 4, CLASSES], BF16)
         nc.sync.dma_start(out=leaf_sb[:], in_=leaf_logits.rearrange("(p t) c -> p t c", t=4))
-
-        bias_sel = setup.tile([P, LOW_TILES, P], F32)
-        nc.vector.tensor_copy(out=bias_sel[:, 0, :], in_=bias_row[:, 127:255])
-        nc.vector.tensor_copy(out=bias_sel[:, 1:3, :], in_=bias_row[:, 255:511].rearrange("p (m c) -> p c m", c=2))
-        bias_t = psum.tile([P, LOW_TILES, P], F32, tag="bank")
-        for nt in range(LOW_TILES):
-            nc.tensor.transpose(bias_t[:, nt, :], bias_sel[:, nt, :], ident[:])
-        bias_pos = const.tile([P, LOW_TILES], F32)
-        nc.vector.tensor_copy(out=bias_pos[:], in_=bias_t[:, :, 0])
-        bias_neg = const.tile([P, LOW_TILES], F32)
-        nc.vector.tensor_scalar_mul(out=bias_neg[:], in0=bias_t[:, :, 0], scalar1=-1.0)
-
-        w_top = const.tile([P, WORD_BLOCKS, 2, TOP], BF16)
-        nc.vector.tensor_copy(out=w_top[:], in_=w_view[:, :, :, 0:TOP])
-        w_grouped = setup.tile([P, PASSES, LOW_TILES, 4 * P], BF16, align_bytes=64)
-        w_codes = const.tile([P, PASSES, LOW_TILES, P], U32, align_bytes=64)
-        w_scales = const.tile([P, PASSES, LOW_TILES, P], U8, align_bytes=64)
-        low_columns = [slice(127, 255), slice(255, 511, 2), slice(256, 511, 2)]
-        for g in range(PASSES):
-            for nt in range(LOW_TILES):
-                nc.vector.tensor_copy(
-                    out=w_grouped[:, g, nt, :].rearrange("p (m u e) -> p m u e", u=2, e=2),
-                    in_=w_view[:, 2 * g : 2 * g + 2, :, low_columns[nt]].rearrange("p u e m -> p m u e"),
-                )
-        leaf_grouped = setup.tile([P, CLASSES, 4], BF16, align_bytes=64)
-        nc.vector.tensor_copy(out=leaf_grouped[:], in_=leaf_sb[:].rearrange("p t c -> p c t"))
-        for g in range(PASSES):
-            for nt in range(LOW_TILES):
-                nc.vector.quantize_mx(
-                    out=w_codes[:, g, nt, :].bitcast(FP8X4), scales=w_scales[:, g, nt, :], in_=w_grouped[:, g, nt, :]
-                )
-        leaf_codes = const.tile([P, CLASSES], U32, align_bytes=64)
-        leaf_scales = const.tile([P, CLASSES], U8, align_bytes=64)
-        nc.vector.quantize_mx(
-            out=leaf_codes[:].bitcast(FP8X4), scales=leaf_scales[:], in_=leaf_grouped[:].rearrange("p c t -> p (c t)")
-        )
+        load_x(2)
 
         grouped_of = {}
         codes_of = {}
@@ -289,24 +262,63 @@ def tile_treemodel_t_kernel(tc, x, w_gate, b_gate, leaf_logits, out):
             nc.scalar.copy(out=result[:], in_=acc[:].rearrange("p r c -> p (r c)"))
             nc.sync.dma_start(out=out_chunks[c], in_=result[:])
 
-        for j in range(-2, N_CHUNKS + 3):
+        transpose_x(0, [0, 2, 1, 3])
+
+        bias_sel = setup.tile([P, LOW_TILES, P], F32)
+        nc.vector.tensor_copy(out=bias_sel[:, 0, :], in_=bias_row[:, 127:255])
+        nc.vector.tensor_copy(out=bias_sel[:, 1:3, :], in_=bias_row[:, 255:511].rearrange("p (m c) -> p c m", c=2))
+        bias_t = psum.tile([P, LOW_TILES, P], F32, tag="bank")
+        for nt in range(LOW_TILES):
+            nc.tensor.transpose(bias_t[:, nt, :], bias_sel[:, nt, :], ident[:])
+        bias_pos = const.tile([P, LOW_TILES], F32)
+        nc.vector.tensor_copy(out=bias_pos[:], in_=bias_t[:, :, 0])
+        bias_neg = const.tile([P, LOW_TILES], F32)
+        nc.vector.tensor_scalar_mul(out=bias_neg[:], in0=bias_t[:, :, 0], scalar1=-1.0)
+
+        w_top = const.tile([P, WORD_BLOCKS, 2, TOP], BF16)
+        w_grouped = setup.tile([P, PASSES, LOW_TILES, 4 * P], BF16, align_bytes=64)
+        w_codes = const.tile([P, PASSES, LOW_TILES, P], U32, align_bytes=64)
+        w_scales = const.tile([P, PASSES, LOW_TILES, P], U8, align_bytes=64)
+        low_columns = [slice(127, 255), slice(255, 511, 2), slice(256, 511, 2)]
+        for g in range(PASSES):
+            nc.vector.tensor_copy(out=w_top[:, 2 * g : 2 * g + 2], in_=w_views[g][:, :, :, 0:TOP])
+            copy = nc.vector.tensor_copy if g == 0 else nc.scalar.copy
+            for nt in range(LOW_TILES):
+                copy(
+                    out=w_grouped[:, g, nt, :].rearrange("p (m u e) -> p m u e", u=2, e=2),
+                    in_=w_views[g][:, :, :, low_columns[nt]].rearrange("p u e m -> p m u e"),
+                )
+        for g in range(PASSES):
+            if g == 1:
+                quantise_x(0)
+            for nt in range(LOW_TILES):
+                nc.vector.quantize_mx(
+                    out=w_codes[:, g, nt, :].bitcast(FP8X4), scales=w_scales[:, g, nt, :], in_=w_grouped[:, g, nt, :]
+                )
+        leaf_grouped = setup.tile([P, CLASSES, 4], BF16, align_bytes=64)
+        nc.vector.tensor_copy(out=leaf_grouped[:], in_=leaf_sb[:].rearrange("p t c -> p c t"))
+        leaf_codes = const.tile([P, CLASSES], U32, align_bytes=64)
+        leaf_scales = const.tile([P, CLASSES], U8, align_bytes=64)
+        nc.vector.quantize_mx(
+            out=leaf_codes[:].bitcast(FP8X4), scales=leaf_scales[:], in_=leaf_grouped[:].rearrange("p c t -> p (c t)")
+        )
+
+        for j in range(N_CHUNKS + 2):
             load_x(j + 3)
-            transpose_x(j + 2, [0, 1])
-            top_gates(j, [0, 1])
-            transpose_x(j + 2, [2, 3])
-            transpose_reach7(j - 2)
-            top_gates(j, [2, 3])
+            top_gates(j, [0, 1, 2, 3])
+            transpose_x(j + 1, [0, 2, 1, 3])
+            transpose_reach7(j - 1)
             low_gates(j)
-            tree_level(j - 1, 1)
-            quantise_probs(j - 3)
-            tree_level(j - 1, 2)
+            tree_level(j, 1)
+            level7_right(j - 1)
+            tree_level(j, 2)
+            level7_left(j - 1)
+            tree_level(j, 3)
             quantise_x(j + 1)
-            tree_level(j - 1, 3)
-            level7_right(j - 2)
-            tree_level(j - 1, 4)
-            level7_left(j - 2)
-            tree_level(j - 1, 5)
-            level8(j - 2, 0)
-            tree_level(j - 1, 6)
-            level8(j - 2, 1)
-            leaves(j - 3)
+            tree_level(j, 4)
+            level8(j - 1, 0)
+            tree_level(j, 5)
+            level8(j - 1, 1)
+            tree_level(j, 6)
+            quantise_probs(j - 1)
+            leaves(j - 2)

@@ -18,8 +18,9 @@ LEAVES = 512
 CLASSES = 128
 TOP = 128
 ROWS = 4
-CHUNK = P * ROWS
-N_CHUNKS = BATCH // CHUNK
+CHUNK_ROWS = [2] + [4] * 15 + [2]
+N_CHUNKS = len(CHUNK_ROWS)
+HALF = 2 * P
 WORD_BLOCKS = 4
 PASSES = 2
 LOW_TILES = 3
@@ -29,8 +30,11 @@ FLOPS = 2 * BATCH * FEATURES * (TOP + NODES - TOP + 1) + 2 * BATCH * LEAVES * CL
 
 def tile_treemodel_t_kernel(tc, x, w_gate, b_gate, leaf_logits, out):
     nc = tc.nc
-    x_chunks = x.rearrange("(i p r) k -> i p (r k)", p=P, r=ROWS)
-    out_chunks = out.rearrange("(i p r) c -> i p (r c)", p=P, r=ROWS)
+
+    def of_chunk(hbm, c):
+        first = P * sum(CHUNK_ROWS[:c])
+        rows = CHUNK_ROWS[c]
+        return hbm[first : first + P * rows, :].rearrange("(p r) k -> p (r k)", r=rows)
 
     with tc.tile_pool(name="const", bufs=1) as const, tc.tile_pool(name="setup", bufs=1) as setup, tc.tile_pool(
         name="two", bufs=2
@@ -46,12 +50,8 @@ def tile_treemodel_t_kernel(tc, x, w_gate, b_gate, leaf_logits, out):
         def load_x(c):
             if not live(c):
                 return
-            x_sb = three.tile([P, ROWS * FEATURES], BF16)
-            parts = 2 if c == 0 else 1
-            width = ROWS * FEATURES // parts
-            for i in range(parts):
-                columns = slice(i * width, (i + 1) * width)
-                nc.sync.dma_start(out=x_sb[:, columns], in_=x_chunks[c][:, columns])
+            x_sb = three.tile([P, CHUNK_ROWS[c] * FEATURES], BF16)
+            nc.sync.dma_start(out=x_sb[:], in_=of_chunk(x, c))
             x_of[c] = x_sb
 
         ident = const.tile([P, P], F32)
@@ -87,99 +87,103 @@ def tile_treemodel_t_kernel(tc, x, w_gate, b_gate, leaf_logits, out):
         probs_of = {}
         p_codes_of = {}
 
-        def transpose_x(c, quarters):
-            if not live(c):
+        def transpose_x(c, bank):
+            if not live(c) or bank >= CHUNK_ROWS[c]:
                 return
-            if quarters[0] == 0:
-                grouped = three.tile([P, PASSES * CHUNK * 4], BF16, align_bytes=64)
+            rows = CHUNK_ROWS[c]
+            h, g = bank // PASSES, bank % PASSES
+            if bank == 0:
+                grouped = three.tile([P, PASSES * rows * P * 4], BF16, align_bytes=64)
                 grouped_of[c] = grouped
-            x_words = x_of[c][:].bitcast(F32).rearrange("p (r w j) -> p r w j", r=ROWS, w=WORD_BLOCKS)
-            grouped_words = grouped_of[c][:].bitcast(F32).rearrange("p (g h b u) -> p g h b u", g=PASSES, h=2, u=2)
-            for q in quarters:
-                g, h = q // 2, q % 2
-                xt = psum.tile([P, 2, CHUNK // 2], F32, tag="bank")
-                for u in range(2):
-                    for r in range(2):
-                        nc.tensor.transpose(
-                            xt[:, u, r * P : (r + 1) * P], x_words[:, 2 * h + r, 2 * g + u, :], ident[:]
-                        )
-                nc.scalar.copy(out=grouped_words[:, g, h], in_=xt[:].rearrange("p u b -> p b u"))
+            x_words = x_of[c][:].bitcast(F32).rearrange("p (r w j) -> p r w j", r=rows, w=WORD_BLOCKS)
+            grouped_words = (
+                grouped_of[c][:].bitcast(F32).rearrange("p (g h b u) -> p g h b u", g=PASSES, h=rows // 2, u=2)
+            )
+            xt = psum.tile([P, 2, HALF], F32, tag="bank")
+            for u in range(2):
+                for r in range(2):
+                    nc.tensor.transpose(xt[:, u, r * P : (r + 1) * P], x_words[:, 2 * h + r, 2 * g + u, :], ident[:])
+            nc.scalar.copy(out=grouped_words[:, g, h], in_=xt[:].rearrange("p u b -> p b u"))
 
         def quantise_x(c):
             if not live(c):
                 return
-            x_codes = three.tile([P, PASSES * CHUNK], U32, align_bytes=64)
-            x_scales = three.tile([P, PASSES * CHUNK], U8, align_bytes=64)
+            chunk = CHUNK_ROWS[c] * P
+            x_codes = three.tile([P, PASSES * chunk], U32, align_bytes=64)
+            x_scales = three.tile([P, PASSES * chunk], U8, align_bytes=64)
             nc.vector.quantize_mx(out=x_codes[:].bitcast(FP8X4), scales=x_scales[:], in_=grouped_of[c][:])
             codes_of[c] = (x_codes, x_scales)
 
-        def top_gates(c, rows):
-            if not live(c):
+        def top_gates(c, r):
+            if not live(c) or r >= CHUNK_ROWS[c]:
                 return
-            if rows[0] == 0:
+            rows = CHUNK_ROWS[c]
+            if r == 0:
                 z_top = psum.tile([P, ROWS, TOP], F32, tag="bank")
                 z_top_of[c] = z_top
             z_top = z_top_of[c]
             grouped_view = grouped_of[c][:].rearrange("p (g b u e) -> p g u b e", g=PASSES, u=2, e=2)
-            for r in rows:
-                nc.tensor.matmul(out=z_top[:, r, :], lhsT=ones[:], rhs=bias_row[:, 0:TOP], start=True, stop=False)
-                for w in range(WORD_BLOCKS):
-                    for e in range(2):
-                        nc.tensor.matmul(
-                            out=z_top[:, r, :],
-                            lhsT=grouped_view[:, w // 2, w % 2, r * P : (r + 1) * P, e],
-                            rhs=w_top[:, w, e, :],
-                            start=False,
-                            stop=(w == WORD_BLOCKS - 1 and e == 1),
-                        )
-            if rows[-1] == ROWS - 1:
-                go_top = three.tile([P, 2, ROWS, TOP], F32)
-                nc.scalar.activation(out=go_top[:, 1], in_=z_top[:], func=SIGMOID)
-                nc.scalar.activation(out=go_top[:, 0], in_=z_top[:], func=SIGMOID, scale=-1.0)
+            nc.tensor.matmul(out=z_top[:, r, :], lhsT=ones[:], rhs=bias_row[:, 0:TOP], start=True, stop=False)
+            for w in range(WORD_BLOCKS):
+                for e in range(2):
+                    nc.tensor.matmul(
+                        out=z_top[:, r, :],
+                        lhsT=grouped_view[:, w // 2, w % 2, r * P : (r + 1) * P, e],
+                        rhs=w_top[:, w, e, :],
+                        start=False,
+                        stop=(w == WORD_BLOCKS - 1 and e == 1),
+                    )
+            if r == rows - 1:
+                go_top = three.tile([P, 2, rows, TOP], F32)
+                nc.scalar.activation(out=go_top[:, 1], in_=z_top[:, 0:rows], func=SIGMOID)
+                nc.scalar.activation(out=go_top[:, 0], in_=z_top[:, 0:rows], func=SIGMOID, scale=-1.0)
                 go_top_of[c] = go_top
 
         def low_gates(c):
             if not live(c):
                 return
+            chunk = CHUNK_ROWS[c] * P
             x_codes, x_scales = codes_of[c]
-            right7 = four.tile([P, CHUNK], F32)
-            go8 = four.tile([P, 4, CHUNK], F32)
+            right7 = four.tile([P, chunk], F32)
+            go8 = four.tile([P, 4, chunk], F32)
             for nt in range(LOW_TILES):
-                z_low = psum.tile([P, CHUNK], F32, tag="bank")
+                z_low = psum.tile([P, ROWS * P], F32, tag="bank")
+                z = z_low[:, 0:chunk]
                 for g in range(PASSES):
                     nc.tensor.matmul_mx(
-                        out=z_low[:],
+                        out=z,
                         lhsT=w_codes[:, g, nt, :].bitcast(FP8X4),
                         lhsT_scale=w_scales[:, g, nt, :],
-                        rhs=x_codes[:, g * CHUNK : (g + 1) * CHUNK].bitcast(FP8X4),
-                        rhs_scale=x_scales[:, g * CHUNK : (g + 1) * CHUNK],
+                        rhs=x_codes[:, g * chunk : (g + 1) * chunk].bitcast(FP8X4),
+                        rhs_scale=x_scales[:, g * chunk : (g + 1) * chunk],
                         start=(g == 0),
                         stop=(g == PASSES - 1),
                     )
                 if nt == 0:
-                    nc.scalar.activation(out=right7[:], in_=z_low[:], func=SIGMOID, bias=bias_pos[:, 0:1])
+                    nc.scalar.activation(out=right7[:], in_=z, func=SIGMOID, bias=bias_pos[:, 0:1])
                 else:
                     c1 = nt - 1
                     nc.scalar.activation(
-                        out=go8[:, 2 * c1 + 1, :], in_=z_low[:], func=SIGMOID, bias=bias_pos[:, nt : nt + 1]
+                        out=go8[:, 2 * c1 + 1, :], in_=z, func=SIGMOID, bias=bias_pos[:, nt : nt + 1]
                     )
                     nc.scalar.activation(
-                        out=go8[:, 2 * c1, :], in_=z_low[:], func=SIGMOID, bias=bias_neg[:, nt : nt + 1], scale=-1.0
+                        out=go8[:, 2 * c1, :], in_=z, func=SIGMOID, bias=bias_neg[:, nt : nt + 1], scale=-1.0
                     )
             low_of[c] = (right7, go8)
 
         def tree_level(c, level):
             if not live(c):
                 return
+            rows = CHUNK_ROWS[c]
             go_view = go_top_of[c][:].rearrange("p c r n -> p r n c")
             if level == 1:
                 reach_of[c] = go_view[:, :, 0, :]
             n = 2**level
-            children = three.tile([P, ROWS, n, 2], F32, name="reach%d" % (level + 1))
+            children = three.tile([P, rows, n, 2], F32, name="reach%d" % (level + 1))
             nc.vector.tensor_tensor(
                 out=children[:],
                 in0=go_view[:, :, n - 1 : 2 * n - 1, :],
-                in1=reach_of[c].unsqueeze(3).to_broadcast([P, ROWS, n, 2]),
+                in1=reach_of[c].unsqueeze(3).to_broadcast([P, rows, n, 2]),
                 op=MULT,
             )
             reach_of[c] = children[:].rearrange("p r j c -> p r (j c)")
@@ -187,19 +191,19 @@ def tile_treemodel_t_kernel(tc, x, w_gate, b_gate, leaf_logits, out):
         def transpose_reach7(c):
             if not live(c):
                 return
-            reach7_t = psum.tile([P, CHUNK], F32, tag="bank")
-            for r in range(ROWS):
+            reach7_t = psum.tile([P, ROWS * P], F32, tag="bank")
+            for r in range(CHUNK_ROWS[c]):
                 nc.tensor.transpose(reach7_t[:, r * P : (r + 1) * P], reach_of[c][:, r, :], ident[:])
-            reach7_t_of[c] = reach7_t
+            reach7_t_of[c] = reach7_t[:, 0 : CHUNK_ROWS[c] * P].rearrange("p (b i) -> p b i", i=4)
 
         def level7_right(c):
             if not live(c):
                 return
-            reach8 = two.tile([P, CHUNK // 4, 2, 4], F32)
+            reach8 = two.tile([P, CHUNK_ROWS[c] * P // 4, 2, 4], F32)
             nc.vector.tensor_tensor(
                 out=reach8[:, :, 1, :],
                 in0=low_of[c][0][:].rearrange("p (b i) -> p b i", i=4),
-                in1=reach7_t_of[c][:].rearrange("p (b i) -> p b i", i=4),
+                in1=reach7_t_of[c],
                 op=MULT,
             )
             reach8_of[c] = reach8
@@ -209,33 +213,30 @@ def tile_treemodel_t_kernel(tc, x, w_gate, b_gate, leaf_logits, out):
                 return
             reach8 = reach8_of[c]
             nc.vector.tensor_tensor(
-                out=reach8[:, :, 0, :],
-                in0=reach7_t_of[c][:].rearrange("p (b i) -> p b i", i=4),
-                in1=reach8[:, :, 1, :],
-                op=SUBTRACT,
+                out=reach8[:, :, 0, :], in0=reach7_t_of[c], in1=reach8[:, :, 1, :], op=SUBTRACT
             )
 
         def level8(c, h):
-            if not live(c):
+            if not live(c) or h >= CHUNK_ROWS[c] // 2:
                 return
             if h == 0:
-                probs = two.tile([P, CHUNK, 2, 2], BF16, align_bytes=64)
+                probs = two.tile([P, CHUNK_ROWS[c] * P, 2, 2], BF16, align_bytes=64)
                 probs_of[c] = probs
-            half = CHUNK // 2
-            rows = slice(h * half, (h + 1) * half)
-            groups = slice(h * half // 4, (h + 1) * half // 4)
+            rows = slice(h * HALF, (h + 1) * HALF)
+            groups = slice(h * HALF // 4, (h + 1) * HALF // 4)
             nc.vector.tensor_tensor(
                 out=probs_of[c][:, rows].rearrange("p (b i) c1 c2 -> p b c1 c2 i", i=4),
                 in0=low_of[c][1][:, :, rows].rearrange("p (c1 c2) (b i) -> p b c1 c2 i", c1=2, i=4),
-                in1=reach8_of[c][:, groups].unsqueeze(3).to_broadcast([P, half // 4, 2, 2, 4]),
+                in1=reach8_of[c][:, groups].unsqueeze(3).to_broadcast([P, HALF // 4, 2, 2, 4]),
                 op=MULT,
             )
 
         def quantise_probs(c):
             if not live(c):
                 return
-            p_codes = three.tile([P, CHUNK], U32, align_bytes=64)
-            p_scales = three.tile([P, CHUNK], U8, align_bytes=64)
+            chunk = CHUNK_ROWS[c] * P
+            p_codes = three.tile([P, chunk], U32, align_bytes=64)
+            p_scales = three.tile([P, chunk], U8, align_bytes=64)
             nc.vector.quantize_mx(
                 out=p_codes[:].bitcast(FP8X4),
                 scales=p_scales[:],
@@ -246,9 +247,10 @@ def tile_treemodel_t_kernel(tc, x, w_gate, b_gate, leaf_logits, out):
         def leaves(c):
             if not live(c):
                 return
+            rows = CHUNK_ROWS[c]
             p_codes, p_scales = p_codes_of[c]
             acc = psum.tile([P, ROWS, CLASSES], F32, tag="bank")
-            for r in range(ROWS):
+            for r in range(rows):
                 nc.tensor.matmul_mx(
                     out=acc[:, r, :],
                     lhsT=p_codes[:, r * P : (r + 1) * P].bitcast(FP8X4),
@@ -258,11 +260,12 @@ def tile_treemodel_t_kernel(tc, x, w_gate, b_gate, leaf_logits, out):
                     start=True,
                     stop=True,
                 )
-            result = three.tile([P, ROWS * CLASSES], F32)
-            nc.scalar.copy(out=result[:], in_=acc[:].rearrange("p r c -> p (r c)"))
-            nc.sync.dma_start(out=out_chunks[c], in_=result[:])
+            result = three.tile([P, rows * CLASSES], F32)
+            nc.scalar.copy(out=result[:], in_=acc[:, 0:rows].rearrange("p r c -> p (r c)"))
+            nc.sync.dma_start(out=of_chunk(out, c), in_=result[:])
 
-        transpose_x(0, [0, 2, 1, 3])
+        for bank in range(ROWS):
+            transpose_x(0, bank)
 
         bias_sel = setup.tile([P, LOW_TILES, P], F32)
         nc.vector.tensor_copy(out=bias_sel[:, 0, :], in_=bias_row[:, 127:255])
@@ -303,22 +306,23 @@ def tile_treemodel_t_kernel(tc, x, w_gate, b_gate, leaf_logits, out):
             out=leaf_codes[:].bitcast(FP8X4), scales=leaf_scales[:], in_=leaf_grouped[:].rearrange("p c t -> p (c t)")
         )
 
-        for j in range(N_CHUNKS + 2):
+        for j in range(N_CHUNKS + 3):
             load_x(j + 3)
-            top_gates(j, [0, 1, 2, 3])
-            transpose_x(j + 1, [0, 2, 1, 3])
+            for i in range(ROWS):
+                top_gates(j, i)
+                transpose_x(j + 1, i)
             transpose_reach7(j - 1)
             low_gates(j)
             tree_level(j, 1)
-            level7_right(j - 1)
+            quantise_probs(j - 2)
             tree_level(j, 2)
-            level7_left(j - 1)
-            tree_level(j, 3)
             quantise_x(j + 1)
+            tree_level(j, 3)
+            level7_right(j - 1)
             tree_level(j, 4)
-            level8(j - 1, 0)
+            level7_left(j - 1)
             tree_level(j, 5)
-            level8(j - 1, 1)
+            level8(j - 1, 0)
             tree_level(j, 6)
-            quantise_probs(j - 1)
-            leaves(j - 2)
+            level8(j - 1, 1)
+            leaves(j - 3)

@@ -18,7 +18,7 @@ LEAVES = 512
 CLASSES = 128
 TOP = 128
 ROWS = 4
-CHUNK_ROWS = [2] + [4] * 15 + [2]
+CHUNK_ROWS = [2, 2] + [4] * 15
 N_CHUNKS = len(CHUNK_ROWS)
 HALF = 2 * P
 WORD_BLOCKS = 4
@@ -196,25 +196,38 @@ def tile_treemodel_t_kernel(tc, x, w_gate, b_gate, leaf_logits, out):
                 nc.tensor.transpose(reach7_t[:, r * P : (r + 1) * P], reach_of[c][:, r, :], ident[:])
             reach7_t_of[c] = reach7_t[:, 0 : CHUNK_ROWS[c] * P].rearrange("p (b i) -> p b i", i=4)
 
+        def spans(c):
+            chunk = CHUNK_ROWS[c] * P
+            step = chunk // 2 if c == N_CHUNKS - 1 else chunk
+            return [slice(first, first + step) for first in range(0, chunk, step)]
+
+        def fours(span):
+            return slice(span.start // 4, span.stop // 4)
+
         def level7_right(c):
             if not live(c):
                 return
             reach8 = two.tile([P, CHUNK_ROWS[c] * P // 4, 2, 4], F32)
-            nc.vector.tensor_tensor(
-                out=reach8[:, :, 1, :],
-                in0=low_of[c][0][:].rearrange("p (b i) -> p b i", i=4),
-                in1=reach7_t_of[c],
-                op=MULT,
-            )
+            for span in spans(c):
+                nc.vector.tensor_tensor(
+                    out=reach8[:, fours(span), 1, :],
+                    in0=low_of[c][0][:, span].rearrange("p (b i) -> p b i", i=4),
+                    in1=reach7_t_of[c][:, fours(span)],
+                    op=MULT,
+                )
             reach8_of[c] = reach8
 
         def level7_left(c):
             if not live(c):
                 return
             reach8 = reach8_of[c]
-            nc.vector.tensor_tensor(
-                out=reach8[:, :, 0, :], in0=reach7_t_of[c], in1=reach8[:, :, 1, :], op=SUBTRACT
-            )
+            for span in spans(c):
+                nc.vector.tensor_tensor(
+                    out=reach8[:, fours(span), 0, :],
+                    in0=reach7_t_of[c][:, fours(span)],
+                    in1=reach8[:, fours(span), 1, :],
+                    op=SUBTRACT,
+                )
 
         def level8(c, h):
             if not live(c) or h >= CHUNK_ROWS[c] // 2:
@@ -222,12 +235,11 @@ def tile_treemodel_t_kernel(tc, x, w_gate, b_gate, leaf_logits, out):
             if h == 0:
                 probs = two.tile([P, CHUNK_ROWS[c] * P, 2, 2], BF16, align_bytes=64)
                 probs_of[c] = probs
-            rows = slice(h * HALF, (h + 1) * HALF)
-            groups = slice(h * HALF // 4, (h + 1) * HALF // 4)
+            half = slice(h * HALF, (h + 1) * HALF)
             nc.vector.tensor_tensor(
-                out=probs_of[c][:, rows].rearrange("p (b i) c1 c2 -> p b c1 c2 i", i=4),
-                in0=low_of[c][1][:, :, rows].rearrange("p (c1 c2) (b i) -> p b c1 c2 i", c1=2, i=4),
-                in1=reach8_of[c][:, groups].unsqueeze(3).to_broadcast([P, HALF // 4, 2, 2, 4]),
+                out=probs_of[c][:, half].rearrange("p (b i) c1 c2 -> p b c1 c2 i", i=4),
+                in0=low_of[c][1][:, :, half].rearrange("p (c1 c2) (b i) -> p b c1 c2 i", c1=2, i=4),
+                in1=reach8_of[c][:, fours(half)].unsqueeze(3).to_broadcast([P, HALF // 4, 2, 2, 4]),
                 op=MULT,
             )
 
@@ -237,32 +249,36 @@ def tile_treemodel_t_kernel(tc, x, w_gate, b_gate, leaf_logits, out):
             chunk = CHUNK_ROWS[c] * P
             p_codes = three.tile([P, chunk], U32, align_bytes=64)
             p_scales = three.tile([P, chunk], U8, align_bytes=64)
-            nc.vector.quantize_mx(
-                out=p_codes[:].bitcast(FP8X4),
-                scales=p_scales[:],
-                in_=probs_of[c][:].rearrange("p b c1 c2 -> p (b c1 c2)"),
-            )
+            for span in spans(c):
+                nc.vector.quantize_mx(
+                    out=p_codes[:, span].bitcast(FP8X4),
+                    scales=p_scales[:, span],
+                    in_=probs_of[c][:, span].rearrange("p b c1 c2 -> p (b c1 c2)"),
+                )
             p_codes_of[c] = (p_codes, p_scales)
 
         def leaves(c):
             if not live(c):
                 return
-            rows = CHUNK_ROWS[c]
             p_codes, p_scales = p_codes_of[c]
-            acc = psum.tile([P, ROWS, CLASSES], F32, tag="bank")
-            for r in range(rows):
-                nc.tensor.matmul_mx(
-                    out=acc[:, r, :],
-                    lhsT=p_codes[:, r * P : (r + 1) * P].bitcast(FP8X4),
-                    lhsT_scale=p_scales[:, r * P : (r + 1) * P],
-                    rhs=leaf_codes[:].bitcast(FP8X4),
-                    rhs_scale=leaf_scales[:],
-                    start=True,
-                    stop=True,
-                )
-            result = three.tile([P, rows * CLASSES], F32)
-            nc.scalar.copy(out=result[:], in_=acc[:, 0:rows].rearrange("p r c -> p (r c)"))
-            nc.sync.dma_start(out=of_chunk(out, c), in_=result[:])
+            out_rows = of_chunk(out, c)
+            for span in spans(c):
+                first, rows = span.start // P, (span.stop - span.start) // P
+                acc = psum.tile([P, ROWS, CLASSES], F32, tag="bank")
+                for r in range(rows):
+                    columns = slice((first + r) * P, (first + r + 1) * P)
+                    nc.tensor.matmul_mx(
+                        out=acc[:, r, :],
+                        lhsT=p_codes[:, columns].bitcast(FP8X4),
+                        lhsT_scale=p_scales[:, columns],
+                        rhs=leaf_codes[:].bitcast(FP8X4),
+                        rhs_scale=leaf_scales[:],
+                        start=True,
+                        stop=True,
+                    )
+                result = three.tile([P, rows * CLASSES], F32)
+                nc.scalar.copy(out=result[:], in_=acc[:, 0:rows].rearrange("p r c -> p (r c)"))
+                nc.sync.dma_start(out=out_rows[:, first * CLASSES : (first + rows) * CLASSES], in_=result[:])
 
         for bank in range(ROWS):
             transpose_x(0, bank)
@@ -285,8 +301,8 @@ def tile_treemodel_t_kernel(tc, x, w_gate, b_gate, leaf_logits, out):
         low_columns = [slice(127, 255), slice(255, 511, 2), slice(256, 511, 2)]
         for g in range(PASSES):
             nc.vector.tensor_copy(out=w_top[:, 2 * g : 2 * g + 2], in_=w_views[g][:, :, :, 0:TOP])
-            copy = nc.vector.tensor_copy if g == 0 else nc.scalar.copy
             for nt in range(LOW_TILES):
+                copy = nc.scalar.copy if g == 1 and nt > 0 else nc.vector.tensor_copy
                 copy(
                     out=w_grouped[:, g, nt, :].rearrange("p (m u e) -> p m u e", u=2, e=2),
                     in_=w_views[g][:, :, :, low_columns[nt]].rearrange("p u e m -> p m u e"),
@@ -299,12 +315,16 @@ def tile_treemodel_t_kernel(tc, x, w_gate, b_gate, leaf_logits, out):
                     out=w_codes[:, g, nt, :].bitcast(FP8X4), scales=w_scales[:, g, nt, :], in_=w_grouped[:, g, nt, :]
                 )
         leaf_grouped = setup.tile([P, CLASSES, 4], BF16, align_bytes=64)
-        nc.vector.tensor_copy(out=leaf_grouped[:], in_=leaf_sb[:].rearrange("p t c -> p c t"))
         leaf_codes = const.tile([P, CLASSES], U32, align_bytes=64)
         leaf_scales = const.tile([P, CLASSES], U8, align_bytes=64)
-        nc.vector.quantize_mx(
-            out=leaf_codes[:].bitcast(FP8X4), scales=leaf_scales[:], in_=leaf_grouped[:].rearrange("p c t -> p (c t)")
-        )
+
+        def quantise_leaves():
+            nc.vector.tensor_copy(out=leaf_grouped[:], in_=leaf_sb[:].rearrange("p t c -> p c t"))
+            nc.vector.quantize_mx(
+                out=leaf_codes[:].bitcast(FP8X4),
+                scales=leaf_scales[:],
+                in_=leaf_grouped[:].rearrange("p c t -> p (c t)"),
+            )
 
         for j in range(N_CHUNKS + 3):
             load_x(j + 3)
@@ -313,14 +333,16 @@ def tile_treemodel_t_kernel(tc, x, w_gate, b_gate, leaf_logits, out):
                 transpose_x(j + 1, i)
             transpose_reach7(j - 1)
             low_gates(j)
+            if j == 1:
+                quantise_leaves()
             tree_level(j, 1)
-            quantise_probs(j - 2)
-            tree_level(j, 2)
-            quantise_x(j + 1)
-            tree_level(j, 3)
             level7_right(j - 1)
-            tree_level(j, 4)
+            tree_level(j, 2)
             level7_left(j - 1)
+            tree_level(j, 3)
+            quantise_probs(j - 2)
+            tree_level(j, 4)
+            quantise_x(j + 1)
             tree_level(j, 5)
             level8(j - 1, 0)
             tree_level(j, 6)

@@ -330,7 +330,9 @@ def tile_treemodel_t_kernel(tc, x, w_gate, b_gate, leaf_logits, out):
             load_x(j + 3)
             for i in range(ROWS):
                 top_gates(j, i)
-                transpose_x(j + 1, i)
+                if i % 2 == 1:
+                    transpose_x(j + 1, i - 1)
+                    transpose_x(j + 1, i)
             transpose_reach7(j - 1)
             low_gates(j)
             if j == 1:
@@ -338,9 +340,9 @@ def tile_treemodel_t_kernel(tc, x, w_gate, b_gate, leaf_logits, out):
             tree_level(j, 1)
             level7_right(j - 1)
             tree_level(j, 2)
-            level7_left(j - 1)
-            tree_level(j, 3)
             quantise_probs(j - 2)
+            tree_level(j, 3)
+            level7_left(j - 1)
             tree_level(j, 4)
             quantise_x(j + 1)
             tree_level(j, 5)

@@ -9,6 +9,7 @@ FP8X4 = mybir.dt.float8_e4m3fn_x4
 SIGMOID = mybir.ActivationFunctionType.Sigmoid
 MULT = mybir.AluOpType.mult
 SUBTRACT = mybir.AluOpType.subtract
+ADD = mybir.AluOpType.add
 
 P = 128
 BATCH = 8192
@@ -23,6 +24,7 @@ N_CHUNKS = len(CHUNK_ROWS)
 HALF = 2 * P
 WORD_BLOCKS = 4
 PASSES = 2
+UPPER = 63
 LOW_TILES = 3
 
 FLOPS = 2 * BATCH * FEATURES * (TOP + NODES - TOP + 1) + 2 * BATCH * LEAVES * CLASSES
@@ -136,7 +138,17 @@ def tile_treemodel_t_kernel(tc, x, w_gate, b_gate, leaf_logits, out):
             if r == rows - 1:
                 go_top = three.tile([P, 2, rows, TOP], F32)
                 nc.scalar.activation(out=go_top[:, 1], in_=z_top[:, 0:rows], func=SIGMOID)
-                nc.scalar.activation(out=go_top[:, 0], in_=z_top[:, 0:rows], func=SIGMOID, scale=-1.0)
+                nc.scalar.activation(
+                    out=go_top[:, 0, :, 0:UPPER], in_=z_top[:, 0:rows, 0:UPPER], func=SIGMOID, scale=-1.0
+                )
+                nc.gpsimd.tensor_scalar(
+                    out=go_top[:, 0, :, UPPER:TOP],
+                    in0=go_top[:, 1, :, UPPER:TOP],
+                    scalar1=-1.0,
+                    scalar2=1.0,
+                    op0=MULT,
+                    op1=ADD,
+                )
                 go_top_of[c] = go_top
 
         def low_gates(c):

@@ -64,15 +64,15 @@ def tile_treemodel_t_kernel(tc, x, w_gate, b_gate, leaf_logits, out):
         nc.scalar.activation(out=warm[:], in_=ones[:, 0:1], func=SIGMOID)
 
         load_x(0)
-        bias_row = const.tile([P, LEAVES], BF16)
-        nc.vector.memset(bias_row[:], 0.0)
-        nc.sync.dma_start(out=bias_row[0:1, 0:NODES], in_=b_gate.unsqueeze(0))
         w_hbm = w_gate.rearrange("(w p e) n -> p w (e n)", w=WORD_BLOCKS, p=P, e=2)
         w_views = []
         for g in range(PASSES):
             w_sb = setup.tile([P, 2, 2 * NODES], BF16, name="w_sb%d" % g)
             nc.sync.dma_start(out=w_sb[:], in_=w_hbm[:, 2 * g : 2 * g + 2])
             w_views.append(w_sb[:].rearrange("p u (e n) -> p u e n", e=2))
+        bias_row = const.tile([P, LEAVES], BF16)
+        nc.vector.memset(bias_row[:], 0.0)
+        nc.sync.dma_start(out=bias_row[0:1, 0:NODES], in_=b_gate.unsqueeze(0))
         load_x(1)
         leaf_sb = setup.tile([P, 4, CLASSES], BF16)
         nc.sync.dma_start(out=leaf_sb[:], in_=leaf_logits.rearrange("(p t) c -> p t c", t=4))
@@ -125,16 +125,16 @@ def tile_treemodel_t_kernel(tc, x, w_gate, b_gate, leaf_logits, out):
                 z_top_of[c] = z_top
             z_top = z_top_of[c]
             grouped_view = grouped_of[c][:].rearrange("p (g b u e) -> p g u b e", g=PASSES, u=2, e=2)
-            nc.tensor.matmul(out=z_top[:, r, :], lhsT=ones[:], rhs=bias_row[:, 0:TOP], start=True, stop=False)
             for w in range(WORD_BLOCKS):
                 for e in range(2):
                     nc.tensor.matmul(
                         out=z_top[:, r, :],
                         lhsT=grouped_view[:, w // 2, w % 2, r * P : (r + 1) * P, e],
                         rhs=w_top[:, w, e, :],
-                        start=False,
-                        stop=(w == WORD_BLOCKS - 1 and e == 1),
+                        start=(w == 0 and e == 0),
+                        stop=False,
                     )
+            nc.tensor.matmul(out=z_top[:, r, :], lhsT=ones[:], rhs=bias_row[:, 0:TOP], start=False, stop=True)
             if r == rows - 1:
                 go_top = three.tile([P, 2, rows, TOP], F32)
                 nc.scalar.activation(out=go_top[:, 1], in_=z_top[:, 0:rows], func=SIGMOID)
@@ -295,17 +295,6 @@ def tile_treemodel_t_kernel(tc, x, w_gate, b_gate, leaf_logits, out):
         for bank in range(ROWS):
             transpose_x(0, bank)
 
-        bias_sel = setup.tile([P, LOW_TILES, P], F32)
-        nc.vector.tensor_copy(out=bias_sel[:, 0, :], in_=bias_row[:, 127:255])
-        nc.vector.tensor_copy(out=bias_sel[:, 1:3, :], in_=bias_row[:, 255:511].rearrange("p (m c) -> p c m", c=2))
-        bias_t = psum.tile([P, LOW_TILES, P], F32, tag="bank")
-        for nt in range(LOW_TILES):
-            nc.tensor.transpose(bias_t[:, nt, :], bias_sel[:, nt, :], ident[:])
-        bias_pos = const.tile([P, LOW_TILES], F32)
-        nc.vector.tensor_copy(out=bias_pos[:], in_=bias_t[:, :, 0])
-        bias_neg = const.tile([P, LOW_TILES], F32)
-        nc.vector.tensor_scalar_mul(out=bias_neg[:], in0=bias_t[:, :, 0], scalar1=-1.0)
-
         w_top = const.tile([P, WORD_BLOCKS, 2, TOP], BF16)
         w_grouped = setup.tile([P, PASSES, LOW_TILES, 4 * P], BF16, align_bytes=64)
         w_codes = const.tile([P, PASSES, LOW_TILES, P], U32, align_bytes=64)
@@ -319,6 +308,9 @@ def tile_treemodel_t_kernel(tc, x, w_gate, b_gate, leaf_logits, out):
                     out=w_grouped[:, g, nt, :].rearrange("p (m u e) -> p m u e", u=2, e=2),
                     in_=w_views[g][:, :, :, low_columns[nt]].rearrange("p u e m -> p m u e"),
                 )
+        bias_sel = setup.tile([P, LOW_TILES, P], F32)
+        nc.vector.tensor_copy(out=bias_sel[:, 0, :], in_=bias_row[:, 127:255])
+        nc.vector.tensor_copy(out=bias_sel[:, 1:3, :], in_=bias_row[:, 255:511].rearrange("p (m c) -> p c m", c=2))
         for g in range(PASSES):
             if g == 1:
                 quantise_x(0)
@@ -338,10 +330,22 @@ def tile_treemodel_t_kernel(tc, x, w_gate, b_gate, leaf_logits, out):
                 in_=leaf_grouped[:].rearrange("p c t -> p (c t)"),
             )
 
+        bias_pos = const.tile([P, LOW_TILES], F32)
+        bias_neg = const.tile([P, LOW_TILES], F32)
+
+        def transpose_biases():
+            bias_t = psum.tile([P, LOW_TILES, P], F32, tag="bank")
+            for nt in range(LOW_TILES):
+                nc.tensor.transpose(bias_t[:, nt, :], bias_sel[:, nt, :], ident[:])
+            nc.vector.tensor_copy(out=bias_pos[:], in_=bias_t[:, :, 0])
+            nc.vector.tensor_scalar_mul(out=bias_neg[:], in0=bias_t[:, :, 0], scalar1=-1.0)
+
         for j in range(N_CHUNKS + 3):
             load_x(j + 3)
             for i in range(ROWS):
                 top_gates(j, i)
+                if j == 0 and i == 1:
+                    transpose_biases()
                 if i % 2 == 1:
                     transpose_x(j + 1, i - 1)
                     transpose_x(j + 1, i)

import concourse.mybir as mybir
from concourse.masks import make_identity

F32 = mybir.dt.float32
BF16 = mybir.dt.bfloat16
U32 = mybir.dt.uint32
U8 = mybir.dt.uint8
FP8X4 = mybir.dt.float8_e4m3fn_x4
SIGMOID = mybir.ActivationFunctionType.Sigmoid
MULT = mybir.AluOpType.mult
SUBTRACT = mybir.AluOpType.subtract
ADD = mybir.AluOpType.add

P = 128
BATCH = 8192
FEATURES = 1024
NODES = 511
LEAVES = 512
CLASSES = 128
TOP = 128
ROWS = 4
CHUNK_ROWS = [2, 2] + [4] * 15
N_CHUNKS = len(CHUNK_ROWS)
HALF = 2 * P
WORD_BLOCKS = 4
PASSES = 2
UPPER = 63
LOW_TILES = 3

FLOPS = 2 * BATCH * FEATURES * (TOP + NODES - TOP + 1) + 2 * BATCH * LEAVES * CLASSES


def tile_treemodel_t_kernel(tc, x, w_gate, b_gate, leaf_logits, out):
    nc = tc.nc

    def of_chunk(hbm, c):
        first = P * sum(CHUNK_ROWS[:c])
        rows = CHUNK_ROWS[c]
        return hbm[first : first + P * rows, :].rearrange("(p r) k -> p (r k)", r=rows)

    with tc.tile_pool(name="const", bufs=1) as const, tc.tile_pool(name="setup", bufs=1) as setup, tc.tile_pool(
        name="two", bufs=2
    ) as two, tc.tile_pool(name="three", bufs=3) as three, tc.tile_pool(name="four", bufs=4) as four, tc.psum_pool(
        name="psum", bufs=8
    ) as psum, tc.manual_schedule():

        x_of = {}

        def live(c):
            return 0 <= c < N_CHUNKS

        def load_x(c):
            if not live(c):
                return
            x_sb = three.tile([P, CHUNK_ROWS[c] * FEATURES], BF16)
            nc.sync.dma_start(out=x_sb[:], in_=of_chunk(x, c))
            x_of[c] = x_sb

        ident = const.tile([P, P], F32)
        make_identity(nc, ident[:])
        ones = const.tile([P, P], BF16)
        nc.vector.memset(ones[:], 1.0)
        warm = const.tile([P, 1], F32)
        nc.scalar.activation(out=warm[:], in_=ones[:, 0:1], func=SIGMOID)

        load_x(0)
        w_hbm = w_gate.rearrange("(w p e) n -> p w (e n)", w=WORD_BLOCKS, p=P, e=2)
        w_views = []
        for g in range(PASSES):
            w_sb = setup.tile([P, 2, 2 * NODES], BF16, name="w_sb%d" % g)
            nc.sync.dma_start(out=w_sb[:], in_=w_hbm[:, 2 * g : 2 * g + 2])
            w_views.append(w_sb[:].rearrange("p u (e n) -> p u e n", e=2))
        bias_row = const.tile([P, LEAVES], BF16)
        nc.vector.memset(bias_row[:], 0.0)
        nc.sync.dma_start(out=bias_row[0:1, 0:NODES], in_=b_gate.unsqueeze(0))
        load_x(1)
        leaf_sb = setup.tile([P, 4, CLASSES], BF16)
        nc.sync.dma_start(out=leaf_sb[:], in_=leaf_logits.rearrange("(p t) c -> p t c", t=4))
        load_x(2)

        grouped_of = {}
        codes_of = {}
        z_top_of = {}
        go_top_of = {}
        reach_of = {}
        low_of = {}
        reach7_t_of = {}
        reach8_of = {}
        probs_of = {}
        p_codes_of = {}

        def transpose_x(c, bank):
            if not live(c) or bank >= CHUNK_ROWS[c]:
                return
            rows = CHUNK_ROWS[c]
            h, g = bank // PASSES, bank % PASSES
            if bank == 0:
                grouped = three.tile([P, PASSES * rows * P * 4], BF16, align_bytes=64)
                grouped_of[c] = grouped
            x_words = x_of[c][:].bitcast(F32).rearrange("p (r w j) -> p r w j", r=rows, w=WORD_BLOCKS)
            grouped_words = (
                grouped_of[c][:].bitcast(F32).rearrange("p (g h b u) -> p g h b u", g=PASSES, h=rows // 2, u=2)
            )
            xt = psum.tile([P, 2, HALF], F32, tag="bank")
            for u in range(2):
                for r in range(2):
                    nc.tensor.transpose(xt[:, u, r * P : (r + 1) * P], x_words[:, 2 * h + r, 2 * g + u, :], ident[:])
            nc.scalar.copy(out=grouped_words[:, g, h], in_=xt[:].rearrange("p u b -> p b u"))

        def quantise_x(c):
            if not live(c):
                return
            chunk = CHUNK_ROWS[c] * P
            x_codes = three.tile([P, PASSES * chunk], U32, align_bytes=64)
            x_scales = three.tile([P, PASSES * chunk], U8, align_bytes=64)
            nc.vector.quantize_mx(out=x_codes[:].bitcast(FP8X4), scales=x_scales[:], in_=grouped_of[c][:])
            codes_of[c] = (x_codes, x_scales)

        def top_gates(c, r):
            if not live(c) or r >= CHUNK_ROWS[c]:
                return
            rows = CHUNK_ROWS[c]
            if r == 0:
                z_top = psum.tile([P, ROWS, TOP], F32, tag="bank")
                z_top_of[c] = z_top
            z_top = z_top_of[c]
            grouped_view = grouped_of[c][:].rearrange("p (g b u e) -> p g u b e", g=PASSES, u=2, e=2)
            for w in range(WORD_BLOCKS):
                for e in range(2):
                    nc.tensor.matmul(
                        out=z_top[:, r, :],
                        lhsT=grouped_view[:, w // 2, w % 2, r * P : (r + 1) * P, e],
                        rhs=w_top[:, w, e, :],
                        start=(w == 0 and e == 0),
                        stop=False,
                    )
            nc.tensor.matmul(out=z_top[:, r, :], lhsT=ones[:], rhs=bias_row[:, 0:TOP], start=False, stop=True)
            if r == rows - 1:
                go_top = three.tile([P, 2, rows, TOP], F32)
                nc.scalar.activation(out=go_top[:, 1], in_=z_top[:, 0:rows], func=SIGMOID)
                nc.scalar.activation(
                    out=go_top[:, 0, :, 0:UPPER], in_=z_top[:, 0:rows, 0:UPPER], func=SIGMOID, scale=-1.0
                )
                nc.gpsimd.tensor_scalar(
                    out=go_top[:, 0, :, UPPER:TOP],
                    in0=go_top[:, 1, :, UPPER:TOP],
                    scalar1=-1.0,
                    scalar2=1.0,
                    op0=MULT,
                    op1=ADD,
                )
                go_top_of[c] = go_top

        def low_gates(c):
            if not live(c):
                return
            chunk = CHUNK_ROWS[c] * P
            x_codes, x_scales = codes_of[c]
            right7 = four.tile([P, chunk], F32)
            go8 = four.tile([P, 4, chunk], F32)
            for nt in range(LOW_TILES):
                z_low = psum.tile([P, ROWS * P], F32, tag="bank")
                z = z_low[:, 0:chunk]
                for g in range(PASSES):
                    nc.tensor.matmul_mx(
                        out=z,
                        lhsT=w_codes[:, g, nt, :].bitcast(FP8X4),
                        lhsT_scale=w_scales[:, g, nt, :],
                        rhs=x_codes[:, g * chunk : (g + 1) * chunk].bitcast(FP8X4),
                        rhs_scale=x_scales[:, g * chunk : (g + 1) * chunk],
                        start=(g == 0),
                        stop=(g == PASSES - 1),
                    )
                if nt == 0:
                    nc.scalar.activation(out=right7[:], in_=z, func=SIGMOID, bias=bias_pos[:, 0:1])
                else:
                    c1 = nt - 1
                    nc.scalar.activation(
                        out=go8[:, 2 * c1 + 1, :], in_=z, func=SIGMOID, bias=bias_pos[:, nt : nt + 1]
                    )
                    nc.scalar.activation(
                        out=go8[:, 2 * c1, :], in_=z, func=SIGMOID, bias=bias_neg[:, nt : nt + 1], scale=-1.0
                    )
            low_of[c] = (right7, go8)

        def tree_level(c, level):
            if not live(c):
                return
            rows = CHUNK_ROWS[c]
            go_view = go_top_of[c][:].rearrange("p c r n -> p r n c")
            if level == 1:
                reach_of[c] = go_view[:, :, 0, :]
            n = 2**level
            children = three.tile([P, rows, n, 2], F32, name="reach%d" % (level + 1))
            nc.vector.tensor_tensor(
                out=children[:],
                in0=go_view[:, :, n - 1 : 2 * n - 1, :],
                in1=reach_of[c].unsqueeze(3).to_broadcast([P, rows, n, 2]),
                op=MULT,
            )
            reach_of[c] = children[:].rearrange("p r j c -> p r (j c)")

        def transpose_reach7(c):
            if not live(c):
                return
            reach7_t = psum.tile([P, ROWS * P], F32, tag="bank")
            for r in range(CHUNK_ROWS[c]):
                nc.tensor.transpose(reach7_t[:, r * P : (r + 1) * P], reach_of[c][:, r, :], ident[:])
            reach7_t_of[c] = reach7_t[:, 0 : CHUNK_ROWS[c] * P].rearrange("p (b i) -> p b i", i=4)

        def spans(c):
            chunk = CHUNK_ROWS[c] * P
            step = chunk // 2 if c == N_CHUNKS - 1 else chunk
            return [slice(first, first + step) for first in range(0, chunk, step)]

        def fours(span):
            return slice(span.start // 4, span.stop // 4)

        def level7_right(c):
            if not live(c):
                return
            reach8 = two.tile([P, CHUNK_ROWS[c] * P // 4, 2, 4], F32)
            for span in spans(c):
                nc.vector.tensor_tensor(
                    out=reach8[:, fours(span), 1, :],
                    in0=low_of[c][0][:, span].rearrange("p (b i) -> p b i", i=4),
                    in1=reach7_t_of[c][:, fours(span)],
                    op=MULT,
                )
            reach8_of[c] = reach8

        def level7_left(c):
            if not live(c):
                return
            reach8 = reach8_of[c]
            for span in spans(c):
                nc.vector.tensor_tensor(
                    out=reach8[:, fours(span), 0, :],
                    in0=reach7_t_of[c][:, fours(span)],
                    in1=reach8[:, fours(span), 1, :],
                    op=SUBTRACT,
                )

        def level8(c, h):
            if not live(c) or h >= CHUNK_ROWS[c] // 2:
                return
            if h == 0:
                probs = two.tile([P, CHUNK_ROWS[c] * P, 2, 2], BF16, align_bytes=64)
                probs_of[c] = probs
            half = slice(h * HALF, (h + 1) * HALF)
            nc.vector.tensor_tensor(
                out=probs_of[c][:, half].rearrange("p (b i) c1 c2 -> p b c1 c2 i", i=4),
                in0=low_of[c][1][:, :, half].rearrange("p (c1 c2) (b i) -> p b c1 c2 i", c1=2, i=4),
                in1=reach8_of[c][:, fours(half)].unsqueeze(3).to_broadcast([P, HALF // 4, 2, 2, 4]),
                op=MULT,
            )

        def quantise_probs(c):
            if not live(c):
                return
            chunk = CHUNK_ROWS[c] * P
            p_codes = three.tile([P, chunk], U32, align_bytes=64)
            p_scales = three.tile([P, chunk], U8, align_bytes=64)
            for span in spans(c):
                nc.vector.quantize_mx(
                    out=p_codes[:, span].bitcast(FP8X4),
                    scales=p_scales[:, span],
                    in_=probs_of[c][:, span].rearrange("p b c1 c2 -> p (b c1 c2)"),
                )
            p_codes_of[c] = (p_codes, p_scales)

        def leaves(c):
            if not live(c):
                return
            p_codes, p_scales = p_codes_of[c]
            out_rows = of_chunk(out, c)
            for span in spans(c):
                first, rows = span.start // P, (span.stop - span.start) // P
                acc = psum.tile([P, ROWS, CLASSES], F32, tag="bank")
                for r in range(rows):
                    columns = slice((first + r) * P, (first + r + 1) * P)
                    nc.tensor.matmul_mx(
                        out=acc[:, r, :],
                        lhsT=p_codes[:, columns].bitcast(FP8X4),
                        lhsT_scale=p_scales[:, columns],
                        rhs=leaf_codes[:].bitcast(FP8X4),
                        rhs_scale=leaf_scales[:],
                        start=True,
                        stop=True,
                    )
                result = three.tile([P, rows * CLASSES], F32)
                nc.scalar.copy(out=result[:], in_=acc[:, 0:rows].rearrange("p r c -> p (r c)"))
                nc.sync.dma_start(out=out_rows[:, first * CLASSES : (first + rows) * CLASSES], in_=result[:])

        for bank in range(ROWS):
            transpose_x(0, bank)

        w_top = const.tile([P, WORD_BLOCKS, 2, TOP], BF16)
        w_grouped = setup.tile([P, PASSES, LOW_TILES, 4 * P], BF16, align_bytes=64)
        w_codes = const.tile([P, PASSES, LOW_TILES, P], U32, align_bytes=64)
        w_scales = const.tile([P, PASSES, LOW_TILES, P], U8, align_bytes=64)
        low_columns = [slice(127, 255), slice(255, 511, 2), slice(256, 511, 2)]
        for g in range(PASSES):
            nc.vector.tensor_copy(out=w_top[:, 2 * g : 2 * g + 2], in_=w_views[g][:, :, :, 0:TOP])
            for nt in range(LOW_TILES):
                copy = nc.scalar.copy if g == 1 and nt > 0 else nc.vector.tensor_copy
                copy(
                    out=w_grouped[:, g, nt, :].rearrange("p (m u e) -> p m u e", u=2, e=2),
                    in_=w_views[g][:, :, :, low_columns[nt]].rearrange("p u e m -> p m u e"),
                )
        bias_sel = setup.tile([P, LOW_TILES, P], F32)
        nc.vector.tensor_copy(out=bias_sel[:, 0, :], in_=bias_row[:, 127:255])
        nc.vector.tensor_copy(out=bias_sel[:, 1:3, :], in_=bias_row[:, 255:511].rearrange("p (m c) -> p c m", c=2))
        for g in range(PASSES):
            if g == 1:
                quantise_x(0)
            for nt in range(LOW_TILES):
                nc.vector.quantize_mx(
                    out=w_codes[:, g, nt, :].bitcast(FP8X4), scales=w_scales[:, g, nt, :], in_=w_grouped[:, g, nt, :]
                )
        leaf_grouped = setup.tile([P, CLASSES, 4], BF16, align_bytes=64)
        leaf_codes = const.tile([P, CLASSES], U32, align_bytes=64)
        leaf_scales = const.tile([P, CLASSES], U8, align_bytes=64)

        def quantise_leaves():
            nc.vector.tensor_copy(out=leaf_grouped[:], in_=leaf_sb[:].rearrange("p t c -> p c t"))
            nc.vector.quantize_mx(
                out=leaf_codes[:].bitcast(FP8X4),
                scales=leaf_scales[:],
                in_=leaf_grouped[:].rearrange("p c t -> p (c t)"),
            )

        bias_pos = const.tile([P, LOW_TILES], F32)
        bias_neg = const.tile([P, LOW_TILES], F32)

        def transpose_biases():
            bias_t = psum.tile([P, LOW_TILES, P], F32, tag="bank")
            for nt in range(LOW_TILES):
                nc.tensor.transpose(bias_t[:, nt, :], bias_sel[:, nt, :], ident[:])
            nc.vector.tensor_copy(out=bias_pos[:], in_=bias_t[:, :, 0])
            nc.vector.tensor_scalar_mul(out=bias_neg[:], in0=bias_t[:, :, 0], scalar1=-1.0)

        for j in range(N_CHUNKS + 3):
            load_x(j + 3)
            for i in range(ROWS):
                top_gates(j, i)
                if j == 0 and i == 1:
                    transpose_biases()
                if i % 2 == 1:
                    transpose_x(j + 1, i - 1)
                    transpose_x(j + 1, i)
            transpose_reach7(j - 1)
            low_gates(j)
            if j == 1:
                quantise_leaves()
            tree_level(j, 1)
            level7_right(j - 1)
            tree_level(j, 2)
            quantise_probs(j - 2)
            tree_level(j, 3)
            level7_left(j - 1)
            tree_level(j, 4)
            quantise_x(j + 1)
            tree_level(j, 5)
            level8(j - 1, 0)
            tree_level(j, 6)
            level8(j - 1, 1)
            leaves(j - 3)
